import numpy as np
import ml_dtypes


def mxq(x, axis, fmt="e4m3"):
    dtype, down = {"e4m3": (ml_dtypes.float8_e4m3fn, 7), "e5m2": (ml_dtypes.float8_e5m2, 14)}[fmt]
    v = np.moveaxis(np.asarray(x, np.float32).astype(ml_dtypes.bfloat16).astype(np.float64), axis, -1)
    blocks = v.reshape(v.shape[:-1] + (-1, 32))
    amax = np.abs(blocks).max(-1, keepdims=True)
    byte = np.maximum(np.where(amax > 0, np.frexp(amax)[1] - 1 + 127, 0) - down, 1)
    scale = np.exp2(byte - 127.0)
    codes = (blocks / scale).astype(np.float32).astype(dtype).astype(np.float64)
    return np.moveaxis((codes * scale).reshape(v.shape), -1, axis)


WIDE = False


def mx_kscale(k):
    if not WIDE:
        return np.ones(k)
    levels = np.array([10, -10, 5, -5, 0])
    a = np.random.permutation(np.resize(levels, k // 512 * 4)).reshape(k // 512, 4)
    idx = np.arange(k)
    return np.exp2(a[idx // 512, idx % 128 // 32])


BF16 = ml_dtypes.bfloat16


def bf(x):
    return np.asarray(x, np.float32).astype(BF16)


def f64(x):
    return np.asarray(x).astype(np.float64)


N, IN_F, HID, OUT_F = 2048, 512, 512, 1024


def setup_inputs():
    s = mx_kscale(HID)
    g = 0.1 + 0.9 * np.random.random_sample(N)
    adj = np.random.random_sample((N, N)) * g[:, None] * g[None, :]
    return {"h1": bf(np.random.standard_normal((N, HID)) * s),
            "adj": bf(adj),
            "W2": bf(np.random.standard_normal((OUT_F, HID)) * 0.125 * np.sqrt(N / HID) / s[None, :]),
            "b2": bf(np.random.standard_normal(OUT_F) * 0.1)}


def reference(h1, adj, W2, b2):
    h = (mxq(f64(h1), 1, "e4m3") @ mxq(f64(W2), 1, "e4m3").T) + f64(b2)
    A = f64(adj) + np.eye(N)
    rowsum = A.sum(axis=1)
    r_inv_sqrt = np.power(rowsum, -0.5)
    r_inv_sqrt = np.where(np.isinf(r_inv_sqrt), 0.0, r_inv_sqrt)
    A = r_inv_sqrt[:, None] * A * r_inv_sqrt[None, :]
    return mxq(A, 1, "e4m3") @ mxq(h, 0, "e4m3")

@@ -1,0 +1,196 @@
+from contextlib import ExitStack
+
+import concourse.mybir as mybir
+from concourse.masks import make_identity
+
+F32 = mybir.dt.float32
+BF16 = mybir.dt.bfloat16
+U32 = mybir.dt.uint32
+U8 = mybir.dt.uint8
+FP8X4 = mybir.dt.float8_e4m3fn_x4
+ACT = mybir.ActivationFunctionType
+ALU = mybir.AluOpType
+
+P = 128
+N_NODES = 2048
+HID = 512
+OUT_F = 1024
+NT = N_NODES // P
+NG = NT // 4
+CV = 768
+
+FLOPS = 2 * N_NODES * HID * OUT_F + 2 * N_NODES * N_NODES * OUT_F
+
+
+def tile_gcnlayer_pa_kernel(tc, h1, adj, W2, b2, out):
+    nc = tc.nc
+    with ExitStack() as ctx:
+        keep = ctx.enter_context(tc.tile_pool(name="keep", bufs=1))
+        wide = ctx.enter_context(tc.tile_pool(name="wide", bufs=2))
+        grp = ctx.enter_context(tc.tile_pool(name="grp", bufs=3))
+        tpool = ctx.enter_context(tc.tile_pool(name="tpool", bufs=3))
+        cpool = ctx.enter_context(tc.tile_pool(name="cpool", bufs=3))
+        opool = ctx.enter_context(tc.tile_pool(name="opool", bufs=3))
+        ps_t = ctx.enter_context(tc.psum_pool(name="ps_t", bufs=4))
+        ps_a = ctx.enter_context(tc.psum_pool(name="ps_a", bufs=4))
+
+        warm = keep.tile([P, 1], F32)
+        warm2 = keep.tile([P, 1], F32)
+        nc.vector.memset(warm[:], 1.0)
+        nc.scalar.activation(out=warm2[:], in_=warm[:], func=ACT.Sqrt)
+        ident = keep.tile([P, P], F32)
+        make_identity(nc, ident[:])
+
+        w2n = keep.tile([P, (OUT_F // P) * HID], BF16)
+        nc.sync.dma_start(
+            out=w2n[:].rearrange("p (c k) -> p c k", k=HID),
+            in_=W2.rearrange("(c p) k -> p c k", p=P),
+        )
+        h1n = keep.tile([P, NT * HID], BF16)
+        for g in range(NG):
+            nc.sync.dma_start(
+                out=h1n[:, 4 * g * HID : 4 * (g + 1) * HID].rearrange("p (x k) -> p x k", k=HID),
+                in_=h1[4 * g * P : 4 * (g + 1) * P, :].rearrange("(x p) k -> p x k", p=P),
+            )
+        bias = keep.tile([P, OUT_F], BF16)
+        nc.gpsimd.dma_start(out=bias[:], in_=b2.partition_broadcast(P))
+        adj_sb = keep.tile([P, NT, N_NODES], BF16)
+        for x in range(NT):
+            nc.sync.dma_start(out=adj_sb[:, x, :], in_=adj[x * P : (x + 1) * P, :])
+
+        w2c = keep.tile([P, OUT_F], U32, align_bytes=64)
+        w2s = keep.tile([P, OUT_F], U8, align_bytes=64)
+        h1c = keep.tile([P, N_NODES], U32, align_bytes=64)
+        h1s = keep.tile([P, N_NODES], U8, align_bytes=64)
+
+        def flip_rows(src_words, first_tile, dst_words):
+            tp = ps_t.tile([P, 4, P], F32, tag="tp")
+            for c in range(2):
+                for u in range(2):
+                    col = (first_tile + c) * (HID // 2) + u * P
+                    nc.tensor.transpose(tp[:, 2 * c + u, :], src_words[:, col : col + P], ident[:])
+            nc.scalar.copy(
+                out=dst_words.rearrange("p (c n u) -> p c n u", c=2, u=2),
+                in_=tp[:].rearrange("p (c u) n -> p c n u", c=2),
+            )
+
+        w2g = wide.tile([P, 4 * OUT_F], BF16, tag="wide", align_bytes=64)
+        for b in range(OUT_F // P // 2):
+            flip_rows(w2n[:].bitcast(F32), 2 * b, w2g[:].bitcast(F32)[:, 512 * b : 512 * (b + 1)])
+        nc.vector.quantize_mx(out=w2c[:].bitcast(FP8X4), scales=w2s[:], in_=w2g[:])
+        for g in range(NG):
+            h1g = grp.tile([P, 4 * 512], BF16, tag="grp", align_bytes=64)
+            for b in range(2):
+                flip_rows(h1n[:].bitcast(F32), 4 * g + 2 * b, h1g[:].bitcast(F32)[:, 512 * b : 512 * (b + 1)])
+            nc.vector.quantize_mx(
+                out=h1c[:, 512 * g : 512 * (g + 1)].bitcast(FP8X4),
+                scales=h1s[:, 512 * g : 512 * (g + 1)],
+                in_=h1g[:],
+            )
+
+        hc = keep.tile([P, NG * OUT_F], U32, align_bytes=64)
+        hs = keep.tile([P, NG * OUT_F], U8, align_bytes=64)
+        deg_v = keep.tile([P, NT], F32)
+        deg_s = keep.tile([P, NT], F32)
+        deg = keep.tile([P, NT], F32)
+        root = keep.tile([P, NT], F32)
+        r = keep.tile([P, NT], F32)
+        junk_v = keep.tile([P, CV], BF16)
+        junk_s = keep.tile([P, N_NODES - CV], BF16)
+        adj_i = keep.tile([P, NT, P], F32)
+
+        for g in range(NG):
+            hg = wide.tile([P, 4 * OUT_F], BF16, tag="wide", align_bytes=64)
+            for nb in range(OUT_F // P):
+                acc = ps_a.tile([P, 4, P], F32, tag="acc")
+                for t in range(4):
+                    x = 4 * g + t
+                    nc.tensor.matmul_mx(
+                        out=acc[:, t, :],
+                        lhsT=h1c[:, x * P : (x + 1) * P].bitcast(FP8X4),
+                        lhsT_scale=h1s[:, x * P : (x + 1) * P],
+                        rhs=w2c[:, nb * P : (nb + 1) * P].bitcast(FP8X4),
+                        rhs_scale=w2s[:, nb * P : (nb + 1) * P],
+                        start=True,
+                        stop=True,
+                    )
+                nc.vector.tensor_tensor(
+                    out=hg[:, 512 * nb : 512 * (nb + 1)].rearrange("p (n t) -> p n t", t=4),
+                    in0=acc[:].rearrange("p t n -> p n t"),
+                    in1=bias[:, nb * P : (nb + 1) * P].unsqueeze(2).to_broadcast([P, P, 4]),
+                    op=ALU.add,
+                )
+            nc.vector.quantize_mx(
+                out=hc[:, OUT_F * g : OUT_F * (g + 1)].bitcast(FP8X4),
+                scales=hs[:, OUT_F * g : OUT_F * (g + 1)],
+                in_=hg[:],
+            )
+            for t in range(4):
+                x = 4 * g + t
+                nc.vector.tensor_scalar(
+                    out=junk_v[:],
+                    in0=adj_sb[:, x, 0:CV],
+                    scalar1=1.0,
+                    scalar2=None,
+                    op0=ALU.mult,
+                    op1=ALU.add,
+                    accum_out=deg_v[:, x : x + 1],
+                )
+                nc.scalar.activation(
+                    out=junk_s[:],
+                    in_=adj_sb[:, x, CV:N_NODES],
+                    func=ACT.Copy,
+                    accum_out=deg_s[:, x : x + 1],
+                )
+                nc.gpsimd.tensor_tensor(
+                    out=adj_i[:, x, :], in0=adj_sb[:, x, x * P : (x + 1) * P], in1=ident[:], op=ALU.add
+                )
+            cols = slice(4 * g, 4 * g + 4)
+            nc.vector.scalar_tensor_tensor(
+                out=deg[:, cols], in0=deg_v[:, cols], scalar=1.0, in1=deg_s[:, cols], op0=ALU.add, op1=ALU.add
+            )
+            nc.scalar.activation(out=root[:, cols], in_=deg[:, cols], func=ACT.Sqrt)
+            nc.vector.reciprocal(out=r[:, cols], in_=root[:, cols])
+
+        for x in range(NT):
+            scaled = tpool.tile([P, N_NODES], F32, tag="scaled")
+            nc.scalar.activation(out=scaled[:], in_=adj_sb[:, x, :], func=ACT.Copy, scale=r[:, x : x + 1])
+            nc.gpsimd.tensor_scalar(
+                out=scaled[:, x * P : (x + 1) * P],
+                in0=adj_i[:, x, :],
+                scalar1=r[:, x : x + 1],
+                scalar2=0.0,
+                op0=ALU.mult,
+                op1=ALU.add,
+            )
+            ag = grp.tile([P, 4 * 512], BF16, tag="grp", align_bytes=64)
+            for g in range(NG):
+                tp = ps_t.tile([P, 4, P], F32, tag="tp")
+                for t in range(4):
+                    j = 4 * g + t
+                    nc.tensor.transpose(tp[:, t, :], scaled[:, j * P : (j + 1) * P], ident[:])
+                nc.vector.tensor_tensor(
+                    out=ag[:, 512 * g : 512 * (g + 1)].rearrange("p (i t) -> p i t", t=4),
+                    in0=tp[:].rearrange("p t i -> p i t"),
+                    in1=r[:, 4 * g : 4 * g + 4].unsqueeze(1).to_broadcast([P, P, 4]),
+                    op=ALU.mult,
+                )
+            ac = cpool.tile([P, 512], U32, tag="ac", align_bytes=64)
+            asc = cpool.tile([P, 512], U8, tag="asc", align_bytes=64)
+            nc.vector.quantize_mx(out=ac[:].bitcast(FP8X4), scales=asc[:], in_=ag[:])
+            ot = opool.tile([P, OUT_F], F32, tag="ot")
+            for nh in range(2):
+                acc = ps_a.tile([P, 512], F32, tag="acc")
+                for g in range(NG):
+                    col = OUT_F * g + 512 * nh
+                    nc.tensor.matmul_mx(
+                        out=acc[:],
+                        lhsT=ac[:, g * P : (g + 1) * P].bitcast(FP8X4),
+                        lhsT_scale=asc[:, g * P : (g + 1) * P],
+                        rhs=hc[:, col : col + 512].bitcast(FP8X4),
+                        rhs_scale=hs[:, col : col + 512],
+                        start=(g == 0),
+                        stop=(g == NG - 1),
+                    )
+                nc.scalar.copy(out=ot[:, 512 * nh : 512 * (nh + 1)], in_=acc[:])
+            nc.sync.dma_start(out=out[x * P : (x + 1) * P, :], in_=ot[:])

@@ -17,7 +17,9 @@ HID = 512
 OUT_F = 1024
 NT = N_NODES // P
 NG = NT // 4
-CV = 768
+FOLD_W = 256
+N_FOLD = 6
+FOLDED = FOLD_W * N_FOLD
 
 FLOPS = 2 * N_NODES * HID * OUT_F + 2 * N_NODES * N_NODES * OUT_F
 
@@ -33,38 +35,51 @@ def tile_gcnlayer_pa_kernel(tc, h1, adj, W2, b2, out):
         opool = ctx.enter_context(tc.tile_pool(name="opool", bufs=3))
         ps_t = ctx.enter_context(tc.psum_pool(name="ps_t", bufs=4))
         ps_a = ctx.enter_context(tc.psum_pool(name="ps_a", bufs=4))
+        ctx.enter_context(tc.manual_schedule())
 
         warm = keep.tile([P, 1], F32)
         warm2 = keep.tile([P, 1], F32)
+        ident = keep.tile([P, P], F32)
+        ident_b = keep.tile([P, P], BF16)
+        w2n = keep.tile([P, (OUT_F // P) * HID], BF16)
+        h1n = keep.tile([P, NT * HID], BF16)
+        bias = keep.tile([P, OUT_F], BF16)
+        adj_sb = keep.tile([P, NT, N_NODES], BF16)
+        w2c = keep.tile([P, OUT_F], U32, align_bytes=64)
+        w2s = keep.tile([P, OUT_F], U8, align_bytes=64)
+        h1c = keep.tile([P, N_NODES], U32, align_bytes=64)
+        h1s = keep.tile([P, N_NODES], U8, align_bytes=64)
+        hc = keep.tile([P, NG * OUT_F], U32, align_bytes=64)
+        hs = keep.tile([P, NG * OUT_F], U8, align_bytes=64)
+        deg_p = keep.tile([P, NT], F32)
+        deg_s = keep.tile([P, NT], F32)
+        deg = keep.tile([P, NT], F32)
+        root = keep.tile([P, NT], F32)
+        r = keep.tile([P, NT], F32)
+        junk = keep.tile([P, N_NODES - FOLDED], BF16)
+        adj_i = keep.tile([P, NT, P], F32)
+        live = {}
+
         nc.vector.memset(warm[:], 1.0)
         nc.scalar.activation(out=warm2[:], in_=warm[:], func=ACT.Sqrt)
-        ident = keep.tile([P, P], F32)
         make_identity(nc, ident[:])
+        make_identity(nc, ident_b[:])
 
-        w2n = keep.tile([P, (OUT_F // P) * HID], BF16)
         nc.sync.dma_start(
             out=w2n[:].rearrange("p (c k) -> p c k", k=HID),
             in_=W2.rearrange("(c p) k -> p c k", p=P),
         )
-        h1n = keep.tile([P, NT * HID], BF16)
         for g in range(NG):
             nc.sync.dma_start(
                 out=h1n[:, 4 * g * HID : 4 * (g + 1) * HID].rearrange("p (x k) -> p x k", k=HID),
                 in_=h1[4 * g * P : 4 * (g + 1) * P, :].rearrange("(x p) k -> p x k", p=P),
             )
-        bias = keep.tile([P, OUT_F], BF16)
         nc.gpsimd.dma_start(out=bias[:], in_=b2.partition_broadcast(P))
-        adj_sb = keep.tile([P, NT, N_NODES], BF16)
         for x in range(NT):
             nc.sync.dma_start(out=adj_sb[:, x, :], in_=adj[x * P : (x + 1) * P, :])
 
-        w2c = keep.tile([P, OUT_F], U32, align_bytes=64)
-        w2s = keep.tile([P, OUT_F], U8, align_bytes=64)
-        h1c = keep.tile([P, N_NODES], U32, align_bytes=64)
-        h1s = keep.tile([P, N_NODES], U8, align_bytes=64)
-
         def flip_rows(src_words, first_tile, dst_words):
-            tp = ps_t.tile([P, 4, P], F32, tag="tp")
+            tp = ps_t.tile([P, 4, P], F32, tag="tp", name="tp")
             for c in range(2):
                 for u in range(2):
                     col = (first_tile + c) * (HID // 2) + u * P
@@ -74,86 +89,92 @@ def tile_gcnlayer_pa_kernel(tc, h1, adj, W2, b2, out):
                 in_=tp[:].rearrange("p (c u) n -> p c n u", c=2),
             )
 
-        w2g = wide.tile([P, 4 * OUT_F], BF16, tag="wide", align_bytes=64)
-        for b in range(OUT_F // P // 2):
-            flip_rows(w2n[:].bitcast(F32), 2 * b, w2g[:].bitcast(F32)[:, 512 * b : 512 * (b + 1)])
-        nc.vector.quantize_mx(out=w2c[:].bitcast(FP8X4), scales=w2s[:], in_=w2g[:])
-        for g in range(NG):
-            h1g = grp.tile([P, 4 * 512], BF16, tag="grp", align_bytes=64)
+        def flip_w2():
+            w2g = wide.tile([P, 4 * OUT_F], BF16, tag="wide", name="w2g", align_bytes=64)
+            live["w2g"] = w2g
+            for b in range(OUT_F // P // 2):
+                flip_rows(w2n[:].bitcast(F32), 2 * b, w2g[:].bitcast(F32)[:, 512 * b : 512 * (b + 1)])
+
+        def quant_w2():
+            nc.vector.quantize_mx(out=w2c[:].bitcast(FP8X4), scales=w2s[:], in_=live["w2g"][:])
+
+        def flip_h1(g):
+            h1g = grp.tile([P, 4 * 512], BF16, tag="grp", name="h1g", align_bytes=64)
+            live["h1g", g] = h1g
             for b in range(2):
                 flip_rows(h1n[:].bitcast(F32), 4 * g + 2 * b, h1g[:].bitcast(F32)[:, 512 * b : 512 * (b + 1)])
+
+        def quant_h1(g):
             nc.vector.quantize_mx(
                 out=h1c[:, 512 * g : 512 * (g + 1)].bitcast(FP8X4),
                 scales=h1s[:, 512 * g : 512 * (g + 1)],
-                in_=h1g[:],
+                in_=live["h1g", g][:],
             )
 
-        hc = keep.tile([P, NG * OUT_F], U32, align_bytes=64)
-        hs = keep.tile([P, NG * OUT_F], U8, align_bytes=64)
-        deg_v = keep.tile([P, NT], F32)
-        deg_s = keep.tile([P, NT], F32)
-        deg = keep.tile([P, NT], F32)
-        root = keep.tile([P, NT], F32)
-        r = keep.tile([P, NT], F32)
-        junk_v = keep.tile([P, CV], BF16)
-        junk_s = keep.tile([P, N_NODES - CV], BF16)
-        adj_i = keep.tile([P, NT, P], F32)
-
-        for g in range(NG):
-            hg = wide.tile([P, 4 * OUT_F], BF16, tag="wide", align_bytes=64)
-            for nb in range(OUT_F // P):
-                acc = ps_a.tile([P, 4, P], F32, tag="acc")
-                for t in range(4):
-                    x = 4 * g + t
-                    nc.tensor.matmul_mx(
-                        out=acc[:, t, :],
-                        lhsT=h1c[:, x * P : (x + 1) * P].bitcast(FP8X4),
-                        lhsT_scale=h1s[:, x * P : (x + 1) * P],
-                        rhs=w2c[:, nb * P : (nb + 1) * P].bitcast(FP8X4),
-                        rhs_scale=w2s[:, nb * P : (nb + 1) * P],
-                        start=True,
-                        stop=True,
-                    )
-                nc.vector.tensor_tensor(
-                    out=hg[:, 512 * nb : 512 * (nb + 1)].rearrange("p (n t) -> p n t", t=4),
-                    in0=acc[:].rearrange("p t n -> p n t"),
-                    in1=bias[:, nb * P : (nb + 1) * P].unsqueeze(2).to_broadcast([P, P, 4]),
-                    op=ALU.add,
+        def project(g, nb):
+            if nb == 0:
+                live["hg", g] = wide.tile([P, 4 * OUT_F], BF16, tag="wide", name="hg", align_bytes=64)
+            hg = live["hg", g]
+            acc = ps_a.tile([P, 4, P], F32, tag="acc", name="acc1")
+            for t in range(4):
+                x = 4 * g + t
+                nc.tensor.matmul_mx(
+                    out=acc[:, t, :],
+                    lhsT=h1c[:, x * P : (x + 1) * P].bitcast(FP8X4),
+                    lhsT_scale=h1s[:, x * P : (x + 1) * P],
+                    rhs=w2c[:, nb * P : (nb + 1) * P].bitcast(FP8X4),
+                    rhs_scale=w2s[:, nb * P : (nb + 1) * P],
+                    start=True,
+                    stop=True,
                 )
+            nc.vector.tensor_tensor(
+                out=hg[:, 512 * nb : 512 * (nb + 1)].rearrange("p (n t) -> p n t", t=4),
+                in0=acc[:].rearrange("p t n -> p n t"),
+                in1=bias[:, nb * P : (nb + 1) * P].unsqueeze(2).to_broadcast([P, P, 4]),
+                op=ALU.add,
+            )
+
+        def quant_h(g):
             nc.vector.quantize_mx(
                 out=hc[:, OUT_F * g : OUT_F * (g + 1)].bitcast(FP8X4),
                 scales=hs[:, OUT_F * g : OUT_F * (g + 1)],
-                in_=hg[:],
+                in_=live["hg", g][:],
             )
-            for t in range(4):
-                x = 4 * g + t
-                nc.vector.tensor_scalar(
-                    out=junk_v[:],
-                    in0=adj_sb[:, x, 0:CV],
-                    scalar1=1.0,
-                    scalar2=None,
-                    op0=ALU.mult,
-                    op1=ALU.add,
-                    accum_out=deg_v[:, x : x + 1],
+
+        def row_sums(x):
+            fold = ps_t.tile([P, FOLD_W], F32, tag="tp", name="fold")
+            for c in range(N_FOLD):
+                nc.tensor.matmul(
+                    out=fold[:],
+                    lhsT=ident_b[:],
+                    rhs=adj_sb[:, x, c * FOLD_W : (c + 1) * FOLD_W],
+                    start=(c == 0),
+                    stop=(c == N_FOLD - 1),
                 )
-                nc.scalar.activation(
-                    out=junk_s[:],
-                    in_=adj_sb[:, x, CV:N_NODES],
-                    func=ACT.Copy,
-                    accum_out=deg_s[:, x : x + 1],
-                )
-                nc.gpsimd.tensor_tensor(
-                    out=adj_i[:, x, :], in0=adj_sb[:, x, x * P : (x + 1) * P], in1=ident[:], op=ALU.add
-                )
+            nc.scalar.activation(
+                out=junk[:, 0:FOLD_W], in_=fold[:], func=ACT.Copy, accum_out=deg_p[:, x : x + 1]
+            )
+            nc.scalar.activation(
+                out=junk[:], in_=adj_sb[:, x, FOLDED:N_NODES], func=ACT.Copy, accum_out=deg_s[:, x : x + 1]
+            )
+            nc.gpsimd.tensor_tensor(
+                out=adj_i[:, x, :], in0=adj_sb[:, x, x * P : (x + 1) * P], in1=ident[:], op=ALU.add
+            )
+
+        def degree(g):
             cols = slice(4 * g, 4 * g + 4)
             nc.vector.scalar_tensor_tensor(
-                out=deg[:, cols], in0=deg_v[:, cols], scalar=1.0, in1=deg_s[:, cols], op0=ALU.add, op1=ALU.add
+                out=deg[:, cols], in0=deg_p[:, cols], scalar=1.0, in1=deg_s[:, cols], op0=ALU.add, op1=ALU.add
             )
             nc.scalar.activation(out=root[:, cols], in_=deg[:, cols], func=ACT.Sqrt)
+
+        def inverse(g):
+            cols = slice(4 * g, 4 * g + 4)
             nc.vector.reciprocal(out=r[:, cols], in_=root[:, cols])
 
-        for x in range(NT):
-            scaled = tpool.tile([P, N_NODES], F32, tag="scaled")
+        def scale_rows(x):
+            scaled = tpool.tile([P, N_NODES], F32, tag="scaled", name="scaled")
+            live["scaled", x] = scaled
             nc.scalar.activation(out=scaled[:], in_=adj_sb[:, x, :], func=ACT.Copy, scale=r[:, x : x + 1])
             nc.gpsimd.tensor_scalar(
                 out=scaled[:, x * P : (x + 1) * P],
@@ -163,24 +184,40 @@ def tile_gcnlayer_pa_kernel(tc, h1, adj, W2, b2, out):
                 op0=ALU.mult,
                 op1=ALU.add,
             )
-            ag = grp.tile([P, 4 * 512], BF16, tag="grp", align_bytes=64)
+
+        def flip_adj(x):
+            scaled = live["scaled", x]
             for g in range(NG):
-                tp = ps_t.tile([P, 4, P], F32, tag="tp")
+                tp = ps_t.tile([P, 4, P], F32, tag="tp", name="tpa")
+                live["tp", x, g] = tp
                 for t in range(4):
                     j = 4 * g + t
                     nc.tensor.transpose(tp[:, t, :], scaled[:, j * P : (j + 1) * P], ident[:])
+
+        def scale_cols(x):
+            ag = grp.tile([P, 4 * 512], BF16, tag="grp", name="ag", align_bytes=64)
+            live["ag", x] = ag
+            for g in range(NG):
                 nc.vector.tensor_tensor(
                     out=ag[:, 512 * g : 512 * (g + 1)].rearrange("p (i t) -> p i t", t=4),
-                    in0=tp[:].rearrange("p t i -> p i t"),
+                    in0=live["tp", x, g][:].rearrange("p t i -> p i t"),
                     in1=r[:, 4 * g : 4 * g + 4].unsqueeze(1).to_broadcast([P, P, 4]),
                     op=ALU.mult,
                 )
-            ac = cpool.tile([P, 512], U32, tag="ac", align_bytes=64)
-            asc = cpool.tile([P, 512], U8, tag="asc", align_bytes=64)
-            nc.vector.quantize_mx(out=ac[:].bitcast(FP8X4), scales=asc[:], in_=ag[:])
-            ot = opool.tile([P, OUT_F], F32, tag="ot")
+
+        def quant_adj(x):
+            ac = cpool.tile([P, 512], U32, tag="ac", name="ac", align_bytes=64)
+            asc = cpool.tile([P, 512], U8, tag="asc", name="asc", align_bytes=64)
+            live["ac", x] = ac
+            live["asc", x] = asc
+            nc.vector.quantize_mx(out=ac[:].bitcast(FP8X4), scales=asc[:], in_=live["ag", x][:])
+
+        def propagate(x):
+            ac = live["ac", x]
+            asc = live["asc", x]
             for nh in range(2):
-                acc = ps_a.tile([P, 512], F32, tag="acc")
+                acc = ps_a.tile([P, 512], F32, tag="acc", name="acc2")
+                live["acc", x, nh] = acc
                 for g in range(NG):
                     col = OUT_F * g + 512 * nh
                     nc.tensor.matmul_mx(
@@ -192,5 +229,55 @@ def tile_gcnlayer_pa_kernel(tc, h1, adj, W2, b2, out):
                         start=(g == 0),
                         stop=(g == NG - 1),
                     )
-                nc.scalar.copy(out=ot[:, 512 * nh : 512 * (nh + 1)], in_=acc[:])
+
+        def store(x):
+            ot = opool.tile([P, OUT_F], F32, tag="ot", name="ot")
+            for nh in range(2):
+                nc.scalar.copy(out=ot[:, 512 * nh : 512 * (nh + 1)], in_=live["acc", x, nh][:])
             nc.sync.dma_start(out=out[x * P : (x + 1) * P, :], in_=ot[:])
+
+        flip_w2()
+        flip_h1(0)
+        quant_w2()
+        quant_h1(0)
+        sums_after = {}
+        for x in range(NT):
+            b = min(31, (6 + 3 * x + 1) // 2)
+            sums_after[b] = sums_after.get(b, []) + [x]
+        degree_at = {}
+        inverse_at = {}
+        for b in range(32):
+            g = b // 8
+            nb = b % 8
+            if nb == 2 and g < NG - 1:
+                flip_h1(g + 1)
+            if nb == 6 and g < NG - 1:
+                quant_h1(g + 1)
+            project(g, nb)
+            for x in sums_after.get(b, []):
+                row_sums(x)
+                if x % 4 == 3:
+                    degree_at[b + 2] = x // 4
+                    inverse_at[b + 4] = x // 4
+            if nb == 7:
+                quant_h(g)
+            if b in degree_at:
+                degree(degree_at[b])
+            if b in inverse_at:
+                inverse(inverse_at[b])
+            if b == 28:
+                scale_rows(0)
+            if b == 30:
+                scale_rows(1)
+        flip_adj(0)
+        for x in range(NT):
+            scale_cols(x)
+            quant_adj(x)
+            if x + 2 < NT:
+                scale_rows(x + 2)
+            if x + 1 < NT:
+                flip_adj(x + 1)
+            propagate(x)
+            if x > 0:
+                store(x - 1)
+        store(NT - 1)

@@ -43,7 +43,9 @@ def tile_gcnlayer_pa_kernel(tc, h1, adj, W2, b2, out):
         ident_b = keep.tile([P, P], BF16)
         w2n = keep.tile([P, (OUT_F // P) * HID], BF16)
         h1n = keep.tile([P, NT * HID], BF16)
-        bias = keep.tile([P, OUT_F], BF16)
+        bias = keep.tile([P, OUT_F], F32)
+        b_row = keep.tile([P, OUT_F], BF16)
+        ones_b = keep.tile([P, P], BF16)
         adj_sb = keep.tile([P, NT, N_NODES], BF16)
         w2c = keep.tile([P, OUT_F], U32, align_bytes=64)
         w2s = keep.tile([P, OUT_F], U8, align_bytes=64)
@@ -61,48 +63,78 @@ def tile_gcnlayer_pa_kernel(tc, h1, adj, W2, b2, out):
         live = {}
 
         nc.vector.memset(warm[:], 1.0)
+        nc.vector.memset(b_row[:], 0.0)
+        nc.vector.memset(ones_b[:], 1.0)
         nc.scalar.activation(out=warm2[:], in_=warm[:], func=ACT.Sqrt)
         make_identity(nc, ident[:])
         make_identity(nc, ident_b[:])
 
-        nc.sync.dma_start(
-            out=w2n[:].rearrange("p (c k) -> p c k", k=HID),
-            in_=W2.rearrange("(c p) k -> p c k", p=P),
-        )
-        for g in range(NG):
+        nc.scalar.dma_start(out=b_row[0:1, :], in_=b2.unsqueeze(0))
+
+        def load_h1(g):
             nc.sync.dma_start(
                 out=h1n[:, 4 * g * HID : 4 * (g + 1) * HID].rearrange("p (x k) -> p x k", k=HID),
                 in_=h1[4 * g * P : 4 * (g + 1) * P, :].rearrange("(x p) k -> p x k", p=P),
             )
-        nc.gpsimd.dma_start(out=bias[:], in_=b2.partition_broadcast(P))
+
+        def load_w2(half):
+            nc.sync.dma_start(
+                out=w2n[:, 4 * half * HID : 4 * (half + 1) * HID].rearrange("p (c k) -> p c k", k=HID),
+                in_=W2[4 * half * P : 4 * (half + 1) * P, :].rearrange("(c p) k -> p c k", p=P),
+            )
+
+        load_h1(0)
+        load_w2(0)
+        load_w2(1)
+        for g in range(1, NG):
+            load_h1(g)
         for x in range(NT):
             nc.sync.dma_start(out=adj_sb[:, x, :], in_=adj[x * P : (x + 1) * P, :])
 
-        def flip_rows(src_words, first_tile, dst_words):
+        def spread_bias():
+            for nh in range(2):
+                pb = ps_a.tile([P, 512], F32, tag="acc", name="pb")
+                nc.tensor.matmul(
+                    out=pb[:], lhsT=ones_b[:], rhs=b_row[:, 512 * nh : 512 * (nh + 1)], start=True, stop=True
+                )
+                nc.vector.tensor_copy(out=bias[:, 512 * nh : 512 * (nh + 1)], in_=pb[:])
+
+        def flip_rows(src_words, first_tile, dst_words, on_vector):
             tp = ps_t.tile([P, 4, P], F32, tag="tp", name="tp")
             for c in range(2):
                 for u in range(2):
                     col = (first_tile + c) * (HID // 2) + u * P
                     nc.tensor.transpose(tp[:, 2 * c + u, :], src_words[:, col : col + P], ident[:])
-            nc.scalar.copy(
-                out=dst_words.rearrange("p (c n u) -> p c n u", c=2, u=2),
-                in_=tp[:].rearrange("p (c u) n -> p c n u", c=2),
+            dst = dst_words.rearrange("p (c n u) -> p c n u", c=2, u=2)
+            src = tp[:].rearrange("p (c u) n -> p c n u", c=2)
+            if on_vector:
+                nc.vector.tensor_copy(out=dst, in_=src)
+            else:
+                nc.scalar.copy(out=dst, in_=src)
+
+        def flip_w2(half, share):
+            if half == 0:
+                live["w2g"] = wide.tile([P, 4 * OUT_F], BF16, tag="wide", name="w2g", align_bytes=64)
+            w2g = live["w2g"]
+            for b in range(2 * half, 2 * half + 2):
+                flip_rows(
+                    w2n[:].bitcast(F32), 2 * b, w2g[:].bitcast(F32)[:, 512 * b : 512 * (b + 1)], share and b % 2 == 1
+                )
+
+        def quant_w2(half):
+            nc.vector.quantize_mx(
+                out=w2c[:, 512 * half : 512 * (half + 1)].bitcast(FP8X4),
+                scales=w2s[:, 512 * half : 512 * (half + 1)],
+                in_=live["w2g"][:, 2048 * half : 2048 * (half + 1)],
             )
 
-        def flip_w2():
-            w2g = wide.tile([P, 4 * OUT_F], BF16, tag="wide", name="w2g", align_bytes=64)
-            live["w2g"] = w2g
-            for b in range(OUT_F // P // 2):
-                flip_rows(w2n[:].bitcast(F32), 2 * b, w2g[:].bitcast(F32)[:, 512 * b : 512 * (b + 1)])
-
-        def quant_w2():
-            nc.vector.quantize_mx(out=w2c[:].bitcast(FP8X4), scales=w2s[:], in_=live["w2g"][:])
-
-        def flip_h1(g):
+        def flip_h1(g, share):
             h1g = grp.tile([P, 4 * 512], BF16, tag="grp", name="h1g", align_bytes=64)
             live["h1g", g] = h1g
             for b in range(2):
-                flip_rows(h1n[:].bitcast(F32), 4 * g + 2 * b, h1g[:].bitcast(F32)[:, 512 * b : 512 * (b + 1)])
+                flip_rows(
+                    h1n[:].bitcast(F32), 4 * g + 2 * b, h1g[:].bitcast(F32)[:, 512 * b : 512 * (b + 1)], share and b == 1
+                )
 
         def quant_h1(g):
             nc.vector.quantize_mx(
@@ -172,10 +204,20 @@ def tile_gcnlayer_pa_kernel(tc, h1, adj, W2, b2, out):
             cols = slice(4 * g, 4 * g + 4)
             nc.vector.reciprocal(out=r[:, cols], in_=root[:, cols])
 
-        def scale_rows(x):
+        def scale_rows(x, on_gpsimd):
             scaled = tpool.tile([P, N_NODES], F32, tag="scaled", name="scaled")
             live["scaled", x] = scaled
-            nc.scalar.activation(out=scaled[:], in_=adj_sb[:, x, :], func=ACT.Copy, scale=r[:, x : x + 1])
+            if on_gpsimd:
+                nc.gpsimd.tensor_scalar(
+                    out=scaled[:],
+                    in0=adj_sb[:, x, :],
+                    scalar1=r[:, x : x + 1],
+                    scalar2=0.0,
+                    op0=ALU.mult,
+                    op1=ALU.add,
+                )
+            else:
+                nc.scalar.activation(out=scaled[:], in_=adj_sb[:, x, :], func=ACT.Copy, scale=r[:, x : x + 1])
             nc.gpsimd.tensor_scalar(
                 out=scaled[:, x * P : (x + 1) * P],
                 in0=adj_i[:, x, :],
@@ -230,54 +272,64 @@ def tile_gcnlayer_pa_kernel(tc, h1, adj, W2, b2, out):
                         stop=(g == NG - 1),
                     )
 
-        def store(x):
+        def store(x, in_halves):
             ot = opool.tile([P, OUT_F], F32, tag="ot", name="ot")
             for nh in range(2):
-                nc.scalar.copy(out=ot[:, 512 * nh : 512 * (nh + 1)], in_=live["acc", x, nh][:])
-            nc.sync.dma_start(out=out[x * P : (x + 1) * P, :], in_=ot[:])
+                cols = slice(512 * nh, 512 * (nh + 1))
+                nc.scalar.copy(out=ot[:, cols], in_=live["acc", x, nh][:])
+                if in_halves:
+                    nc.sync.dma_start(out=out[x * P : (x + 1) * P, cols], in_=ot[:, cols])
+            if not in_halves:
+                nc.sync.dma_start(out=out[x * P : (x + 1) * P, :], in_=ot[:])
 
-        flip_w2()
-        flip_h1(0)
-        quant_w2()
+        spread_bias()
+        flip_h1(0, True)
+        flip_w2(0, True)
         quant_h1(0)
+        quant_w2(0)
         sums_after = {}
         for x in range(NT):
-            b = min(31, (6 + 3 * x + 1) // 2)
+            b = min(31, (50 + 17 * x + 5) // 10)
             sums_after[b] = sums_after.get(b, []) + [x]
         degree_at = {}
         inverse_at = {}
-        for b in range(32):
+        for b in range(37):
             g = b // 8
             nb = b % 8
-            if nb == 2 and g < NG - 1:
-                flip_h1(g + 1)
-            if nb == 6 and g < NG - 1:
-                quant_h1(g + 1)
-            project(g, nb)
-            for x in sums_after.get(b, []):
-                row_sums(x)
-                if x % 4 == 3:
-                    degree_at[b + 2] = x // 4
-                    inverse_at[b + 4] = x // 4
-            if nb == 7:
-                quant_h(g)
+            if b < 32:
+                if b == 0:
+                    flip_w2(1, False)
+                if b == 2:
+                    quant_w2(1)
+                if nb == 3 and g < NG - 1:
+                    flip_h1(g + 1, False)
+                if nb == 6 and g < NG - 1:
+                    quant_h1(g + 1)
+                project(g, nb)
+                for x in sums_after.get(b, []):
+                    row_sums(x)
+                    if x % 4 == 3:
+                        degree_at[b + 3] = x // 4
+                        inverse_at[b + 5] = x // 4
+                if nb == 7:
+                    quant_h(g)
             if b in degree_at:
                 degree(degree_at[b])
             if b in inverse_at:
                 inverse(inverse_at[b])
             if b == 28:
-                scale_rows(0)
+                scale_rows(0, True)
             if b == 30:
-                scale_rows(1)
+                scale_rows(1, True)
         flip_adj(0)
         for x in range(NT):
             scale_cols(x)
             quant_adj(x)
             if x + 2 < NT:
-                scale_rows(x + 2)
+                scale_rows(x + 2, False)
             if x + 1 < NT:
                 flip_adj(x + 1)
             propagate(x)
             if x > 0:
-                store(x - 1)
-        store(NT - 1)
+                store(x - 1, False)
+        store(NT - 1, True)

@@ -69,7 +69,7 @@ def tile_gcnlayer_pa_kernel(tc, h1, adj, W2, b2, out):
         make_identity(nc, ident[:])
         make_identity(nc, ident_b[:])
 
-        nc.scalar.dma_start(out=b_row[0:1, :], in_=b2.unsqueeze(0))
+        nc.sync.dma_start(out=b_row[0:1, :], in_=b2.unsqueeze(0))
 
         def load_h1(g):
             nc.sync.dma_start(
@@ -236,10 +236,11 @@ def tile_gcnlayer_pa_kernel(tc, h1, adj, W2, b2, out):
                     j = 4 * g + t
                     nc.tensor.transpose(tp[:, t, :], scaled[:, j * P : (j + 1) * P], ident[:])
 
-        def scale_cols(x):
-            ag = grp.tile([P, 4 * 512], BF16, tag="grp", name="ag", align_bytes=64)
-            live["ag", x] = ag
-            for g in range(NG):
+        def scale_cols(x, passes):
+            if passes[0] == 0:
+                live["ag", x] = grp.tile([P, 4 * 512], BF16, tag="grp", name="ag", align_bytes=64)
+            ag = live["ag", x]
+            for g in passes:
                 nc.vector.tensor_tensor(
                     out=ag[:, 512 * g : 512 * (g + 1)].rearrange("p (i t) -> p i t", t=4),
                     in0=live["tp", x, g][:].rearrange("p t i -> p i t"),
@@ -282,9 +283,9 @@ def tile_gcnlayer_pa_kernel(tc, h1, adj, W2, b2, out):
             if not in_halves:
                 nc.sync.dma_start(out=out[x * P : (x + 1) * P, :], in_=ot[:])
 
-        spread_bias()
         flip_h1(0, True)
         flip_w2(0, True)
+        spread_bias()
         quant_h1(0)
         quant_w2(0)
         sums_after = {}
@@ -293,7 +294,7 @@ def tile_gcnlayer_pa_kernel(tc, h1, adj, W2, b2, out):
             sums_after[b] = sums_after.get(b, []) + [x]
         degree_at = {}
         inverse_at = {}
-        for b in range(37):
+        for b in range(35):
             g = b // 8
             nb = b % 8
             if b < 32:
@@ -306,13 +307,14 @@ def tile_gcnlayer_pa_kernel(tc, h1, adj, W2, b2, out):
                 if nb == 6 and g < NG - 1:
                     quant_h1(g + 1)
                 project(g, nb)
+                if nb == 0 and g > 0:
+                    quant_h(g - 1)
                 for x in sums_after.get(b, []):
                     row_sums(x)
                     if x % 4 == 3:
                         degree_at[b + 3] = x // 4
-                        inverse_at[b + 5] = x // 4
-                if nb == 7:
-                    quant_h(g)
+                        if x < NT - 1:
+                            inverse_at[b + 5] = x // 4
             if b in degree_at:
                 degree(degree_at[b])
             if b in inverse_at:
@@ -323,10 +325,16 @@ def tile_gcnlayer_pa_kernel(tc, h1, adj, W2, b2, out):
                 scale_rows(1, True)
         flip_adj(0)
         for x in range(NT):
-            scale_cols(x)
+            scale_cols(x, [0])
+            if x == 0:
+                quant_h(NG - 1)
+            scale_cols(x, [1, 2])
+            if x == 0:
+                inverse(NG - 1)
+            scale_cols(x, [3])
             quant_adj(x)
             if x + 2 < NT:
-                scale_rows(x + 2, False)
+                scale_rows(x + 2, (x + 2) % 4 == 1)
             if x + 1 < NT:
                 flip_adj(x + 1)
             propagate(x)

@@ -17,8 +17,8 @@ HID = 512
 OUT_F = 1024
 NT = N_NODES // P
 NG = NT // 4
-FOLD_W = 256
-N_FOLD = 6
+FOLD_W = 128
+N_FOLD = 12
 FOLDED = FOLD_W * N_FOLD
 
 FLOPS = 2 * N_NODES * HID * OUT_F + 2 * N_NODES * N_NODES * OUT_F
@@ -30,7 +30,7 @@ def tile_gcnlayer_pa_kernel(tc, h1, adj, W2, b2, out):
         keep = ctx.enter_context(tc.tile_pool(name="keep", bufs=1))
         wide = ctx.enter_context(tc.tile_pool(name="wide", bufs=2))
         grp = ctx.enter_context(tc.tile_pool(name="grp", bufs=3))
-        tpool = ctx.enter_context(tc.tile_pool(name="tpool", bufs=3))
+        spool = ctx.enter_context(tc.tile_pool(name="spool", bufs=3))
         cpool = ctx.enter_context(tc.tile_pool(name="cpool", bufs=3))
         opool = ctx.enter_context(tc.tile_pool(name="opool", bufs=3))
         ps_t = ctx.enter_context(tc.psum_pool(name="ps_t", bufs=4))
@@ -55,9 +55,8 @@ def tile_gcnlayer_pa_kernel(tc, h1, adj, W2, b2, out):
         hs = keep.tile([P, NG * OUT_F], U8, align_bytes=64)
         deg_p = keep.tile([P, NT], F32)
         deg_s = keep.tile([P, NT], F32)
-        deg = keep.tile([P, NT], F32)
-        root = keep.tile([P, NT], F32)
         r = keep.tile([P, NT], F32)
+        r_row = keep.tile([P, N_NODES], F32)
         junk = keep.tile([P, N_NODES - FOLDED], BF16)
         adj_i = keep.tile([P, NT, P], F32)
         live = {}
@@ -65,7 +64,7 @@ def tile_gcnlayer_pa_kernel(tc, h1, adj, W2, b2, out):
         nc.vector.memset(warm[:], 1.0)
         nc.vector.memset(b_row[:], 0.0)
         nc.vector.memset(ones_b[:], 1.0)
-        nc.scalar.activation(out=warm2[:], in_=warm[:], func=ACT.Sqrt)
+        nc.scalar.activation(out=warm2[:], in_=warm[:], func=ACT.Abs_reciprocal_sqrt)
         make_identity(nc, ident[:])
         make_identity(nc, ident_b[:])
 
@@ -73,8 +72,8 @@ def tile_gcnlayer_pa_kernel(tc, h1, adj, W2, b2, out):
 
         def load_h1(g):
             nc.sync.dma_start(
-                out=h1n[:, 4 * g * HID : 4 * (g + 1) * HID].rearrange("p (x k) -> p x k", k=HID),
-                in_=h1[4 * g * P : 4 * (g + 1) * P, :].rearrange("(x p) k -> p x k", p=P),
+                out=h1n[:, 4 * g * HID : 4 * (g + 1) * HID].rearrange("p (u e k) -> p u e k", u=2, e=2),
+                in_=h1[4 * g * P : 4 * (g + 1) * P, :].rearrange("(u p e) k -> p u e k", p=P, e=2),
             )
 
         def load_w2(half):
@@ -173,6 +172,14 @@ def tile_gcnlayer_pa_kernel(tc, h1, adj, W2, b2, out):
                 in_=live["hg", g][:],
             )
 
+        def inverse_root(x):
+            nc.scalar.activation(
+                out=r[:, x : x + 1],
+                in_=deg_p[:, x : x + 1],
+                func=ACT.Abs_reciprocal_sqrt,
+                bias=deg_s[:, x : x + 1],
+            )
+
         def row_sums(x):
             fold = ps_t.tile([P, FOLD_W], F32, tag="tp", name="fold")
             for c in range(N_FOLD):
@@ -184,68 +191,66 @@ def tile_gcnlayer_pa_kernel(tc, h1, adj, W2, b2, out):
                     stop=(c == N_FOLD - 1),
                 )
             nc.scalar.activation(
-                out=junk[:, 0:FOLD_W], in_=fold[:], func=ACT.Copy, accum_out=deg_p[:, x : x + 1]
+                out=junk[:],
+                in_=adj_sb[:, x, FOLDED:N_NODES],
+                func=ACT.Copy,
+                bias=1.0 / (N_NODES - FOLDED),
+                accum_out=deg_s[:, x : x + 1],
             )
+            if x > 0:
+                inverse_root(x - 1)
             nc.scalar.activation(
-                out=junk[:], in_=adj_sb[:, x, FOLDED:N_NODES], func=ACT.Copy, accum_out=deg_s[:, x : x + 1]
+                out=junk[:, 0:FOLD_W], in_=fold[:], func=ACT.Copy, accum_out=deg_p[:, x : x + 1]
             )
             nc.gpsimd.tensor_tensor(
                 out=adj_i[:, x, :], in0=adj_sb[:, x, x * P : (x + 1) * P], in1=ident[:], op=ALU.add
             )
 
-        def degree(g):
-            cols = slice(4 * g, 4 * g + 4)
+        def spread(g):
+            sp = ps_t.tile([P, 4, P], F32, tag="tp", name="sp")
+            for t in range(4):
+                x = 4 * g + t
+                nc.tensor.transpose(sp[:, t, :], r[:, x : x + 1].to_broadcast([P, P]), ident[:])
+            nc.scalar.copy(
+                out=r_row[:, 512 * g : 512 * (g + 1)].rearrange("p (t n) -> p t n", t=4), in_=sp[:]
+            )
+
+        def scale_piece(x, lo, hi, src):
             nc.vector.scalar_tensor_tensor(
-                out=deg[:, cols], in0=deg_p[:, cols], scalar=1.0, in1=deg_s[:, cols], op0=ALU.add, op1=ALU.add
-            )
-            nc.scalar.activation(out=root[:, cols], in_=deg[:, cols], func=ACT.Sqrt)
-
-        def inverse(g):
-            cols = slice(4 * g, 4 * g + 4)
-            nc.vector.reciprocal(out=r[:, cols], in_=root[:, cols])
-
-        def scale_rows(x, on_gpsimd):
-            scaled = tpool.tile([P, N_NODES], F32, tag="scaled", name="scaled")
-            live["scaled", x] = scaled
-            if on_gpsimd:
-                nc.gpsimd.tensor_scalar(
-                    out=scaled[:],
-                    in0=adj_sb[:, x, :],
-                    scalar1=r[:, x : x + 1],
-                    scalar2=0.0,
-                    op0=ALU.mult,
-                    op1=ALU.add,
-                )
-            else:
-                nc.scalar.activation(out=scaled[:], in_=adj_sb[:, x, :], func=ACT.Copy, scale=r[:, x : x + 1])
-            nc.gpsimd.tensor_scalar(
-                out=scaled[:, x * P : (x + 1) * P],
-                in0=adj_i[:, x, :],
-                scalar1=r[:, x : x + 1],
-                scalar2=0.0,
+                out=live["scaled", x][:, lo:hi],
+                in0=src,
+                scalar=r[:, x : x + 1],
+                in1=r_row[:, lo:hi],
                 op0=ALU.mult,
-                op1=ALU.add,
+                op1=ALU.mult,
             )
+
+        def scale(x):
+            live["scaled", x] = spool.tile([P, N_NODES], BF16, tag="scaled", name="scaled", align_bytes=64)
+            d0 = x * P
+            d1 = d0 + P
+            if x > 0:
+                scale_piece(x, 0, d0, adj_sb[:, x, 0:d0])
+            scale_piece(x, d0, d1, adj_i[:, x, :])
+            if x < NT - 1:
+                scale_piece(x, d1, N_NODES, adj_sb[:, x, d1:N_NODES])
 
         def flip_adj(x):
-            scaled = live["scaled", x]
-            for g in range(NG):
+            words = live["scaled", x][:].bitcast(F32)
+            for b in range(2):
                 tp = ps_t.tile([P, 4, P], F32, tag="tp", name="tpa")
-                live["tp", x, g] = tp
-                for t in range(4):
-                    j = 4 * g + t
-                    nc.tensor.transpose(tp[:, t, :], scaled[:, j * P : (j + 1) * P], ident[:])
+                live["tp", x, b] = tp
+                for c in range(4):
+                    col = (4 * b + c) * P
+                    nc.tensor.transpose(tp[:, c, :], words[:, col : col + P], ident[:])
 
-        def scale_cols(x, passes):
-            if passes[0] == 0:
-                live["ag", x] = grp.tile([P, 4 * 512], BF16, tag="grp", name="ag", align_bytes=64)
-            ag = live["ag", x]
-            for g in passes:
-                nc.vector.tensor_tensor(
-                    out=ag[:, 512 * g : 512 * (g + 1)].rearrange("p (i t) -> p i t", t=4),
-                    in0=live["tp", x, g][:].rearrange("p t i -> p i t"),
-                    in1=r[:, 4 * g : 4 * g + 4].unsqueeze(1).to_broadcast([P, P, 4]),
-                    op=ALU.mult,
+        def regroup(x):
+            ag = grp.tile([P, 4 * 512], BF16, tag="grp", name="ag", align_bytes=64)
+            live["ag", x] = ag
+            for b in range(2):
+                nc.scalar.copy(
+                    out=ag[:].bitcast(F32)[:, 512 * b : 512 * (b + 1)].rearrange("p (g i u) -> p g i u", g=2, u=2),
+                    in_=live["tp", x, b][:].rearrange("p (g u) i -> p g i u", g=2),
                 )
 
         def quant_adj(x):
@@ -292,52 +297,46 @@ def tile_gcnlayer_pa_kernel(tc, h1, adj, W2, b2, out):
         for x in range(NT):
             b = min(31, (50 + 17 * x + 5) // 10)
             sums_after[b] = sums_after.get(b, []) + [x]
-        degree_at = {}
-        inverse_at = {}
-        for b in range(35):
+        spread_at = {}
+        for b in range(32):
             g = b // 8
             nb = b % 8
-            if b < 32:
-                if b == 0:
-                    flip_w2(1, False)
-                if b == 2:
-                    quant_w2(1)
-                if nb == 3 and g < NG - 1:
-                    flip_h1(g + 1, False)
-                if nb == 6 and g < NG - 1:
-                    quant_h1(g + 1)
-                project(g, nb)
-                if nb == 0 and g > 0:
-                    quant_h(g - 1)
-                for x in sums_after.get(b, []):
-                    row_sums(x)
-                    if x % 4 == 3:
-                        degree_at[b + 3] = x // 4
-                        if x < NT - 1:
-                            inverse_at[b + 5] = x // 4
-            if b in degree_at:
-                degree(degree_at[b])
-            if b in inverse_at:
-                inverse(inverse_at[b])
-            if b == 28:
-                scale_rows(0, True)
-            if b == 30:
-                scale_rows(1, True)
+            if b == 0:
+                flip_w2(1, False)
+            if b == 2:
+                quant_w2(1)
+            if nb == 3 and g < NG - 1:
+                flip_h1(g + 1, False)
+            if nb == 6 and g < NG - 1:
+                quant_h1(g + 1)
+            project(g, nb)
+            if nb == 0 and g > 0:
+                quant_h(g - 1)
+            for x in sums_after.get(b, []):
+                row_sums(x)
+                if x % 4 == 0 and x > 0:
+                    spread_at[b + 1] = x // 4 - 1
+            if b in spread_at:
+                spread(spread_at[b])
+        inverse_root(NT - 1)
+        spread(NG - 1)
+        scale(0)
         flip_adj(0)
+        regroup(0)
+        quant_h(NG - 1)
+        scale(1)
+        flip_adj(1)
+        quant_adj(0)
+        regroup(1)
         for x in range(NT):
-            scale_cols(x, [0])
-            if x == 0:
-                quant_h(NG - 1)
-            scale_cols(x, [1, 2])
-            if x == 0:
-                inverse(NG - 1)
-            scale_cols(x, [3])
-            quant_adj(x)
-            if x + 2 < NT:
-                scale_rows(x + 2, (x + 2) % 4 == 1)
-            if x + 1 < NT:
-                flip_adj(x + 1)
             propagate(x)
+            if x + 2 < NT:
+                scale(x + 2)
+                flip_adj(x + 2)
+            if x + 1 < NT:
+                quant_adj(x + 1)
             if x > 0:
                 store(x - 1, False)
+            if x + 2 < NT:
+                regroup(x + 2)
         store(NT - 1, True)

@@ -18,7 +18,7 @@ OUT_F = 1024
 NT = N_NODES // P
 NG = NT // 4
 FOLD_W = 128
-N_FOLD = 12
+N_FOLD = 11
 FOLDED = FOLD_W * N_FOLD
 
 FLOPS = 2 * N_NODES * HID * OUT_F + 2 * N_NODES * N_NODES * OUT_F
@@ -28,8 +28,8 @@ def tile_gcnlayer_pa_kernel(tc, h1, adj, W2, b2, out):
     nc = tc.nc
     with ExitStack() as ctx:
         keep = ctx.enter_context(tc.tile_pool(name="keep", bufs=1))
-        wide = ctx.enter_context(tc.tile_pool(name="wide", bufs=2))
-        grp = ctx.enter_context(tc.tile_pool(name="grp", bufs=3))
+        wide = ctx.enter_context(tc.tile_pool(name="wide", bufs=3))
+        grp = ctx.enter_context(tc.tile_pool(name="grp", bufs=4))
         spool = ctx.enter_context(tc.tile_pool(name="spool", bufs=3))
         cpool = ctx.enter_context(tc.tile_pool(name="cpool", bufs=3))
         opool = ctx.enter_context(tc.tile_pool(name="opool", bufs=3))
@@ -58,6 +58,7 @@ def tile_gcnlayer_pa_kernel(tc, h1, adj, W2, b2, out):
         r = keep.tile([P, NT], F32)
         r_row = keep.tile([P, N_NODES], F32)
         junk = keep.tile([P, N_NODES - FOLDED], BF16)
+        junk2 = keep.tile([P, FOLD_W], BF16)
         adj_i = keep.tile([P, NT, P], F32)
         live = {}
 
@@ -68,7 +69,7 @@ def tile_gcnlayer_pa_kernel(tc, h1, adj, W2, b2, out):
         make_identity(nc, ident[:])
         make_identity(nc, ident_b[:])
 
-        nc.sync.dma_start(out=b_row[0:1, :], in_=b2.unsqueeze(0))
+        nc.scalar.dma_start(out=b_row[0:1, :], in_=b2.unsqueeze(0))
 
         def load_h1(g):
             nc.sync.dma_start(
@@ -82,13 +83,17 @@ def tile_gcnlayer_pa_kernel(tc, h1, adj, W2, b2, out):
                 in_=W2[4 * half * P : 4 * (half + 1) * P, :].rearrange("(c p) k -> p c k", p=P),
             )
 
+        def load_adj(x):
+            nc.sync.dma_start(out=adj_sb[:, x, :], in_=adj[x * P : (x + 1) * P, :])
+
         load_h1(0)
         load_w2(0)
-        load_w2(1)
         for g in range(1, NG):
             load_h1(g)
         for x in range(NT):
-            nc.sync.dma_start(out=adj_sb[:, x, :], in_=adj[x * P : (x + 1) * P, :])
+            load_adj(x)
+            if x == 6:
+                load_w2(1)
 
         def spread_bias():
             for nh in range(2):
@@ -96,7 +101,7 @@ def tile_gcnlayer_pa_kernel(tc, h1, adj, W2, b2, out):
                 nc.tensor.matmul(
                     out=pb[:], lhsT=ones_b[:], rhs=b_row[:, 512 * nh : 512 * (nh + 1)], start=True, stop=True
                 )
-                nc.vector.tensor_copy(out=bias[:, 512 * nh : 512 * (nh + 1)], in_=pb[:])
+                nc.scalar.copy(out=bias[:, 512 * nh : 512 * (nh + 1)], in_=pb[:])
 
         def flip_rows(src_words, first_tile, dst_words, on_vector):
             tp = ps_t.tile([P, 4, P], F32, tag="tp", name="tp")
@@ -112,19 +117,18 @@ def tile_gcnlayer_pa_kernel(tc, h1, adj, W2, b2, out):
                 nc.scalar.copy(out=dst, in_=src)
 
         def flip_w2(half, share):
-            if half == 0:
-                live["w2g"] = wide.tile([P, 4 * OUT_F], BF16, tag="wide", name="w2g", align_bytes=64)
-            w2g = live["w2g"]
-            for b in range(2 * half, 2 * half + 2):
+            w2g = wide.tile([P, 4 * 512], BF16, tag="wide", name="w2g", align_bytes=64)
+            live["w2g", half] = w2g
+            for b in range(2):
                 flip_rows(
-                    w2n[:].bitcast(F32), 2 * b, w2g[:].bitcast(F32)[:, 512 * b : 512 * (b + 1)], share and b % 2 == 1
+                    w2n[:].bitcast(F32), 4 * half + 2 * b, w2g[:].bitcast(F32)[:, 512 * b : 512 * (b + 1)], share and b == 1
                 )
 
         def quant_w2(half):
             nc.vector.quantize_mx(
                 out=w2c[:, 512 * half : 512 * (half + 1)].bitcast(FP8X4),
                 scales=w2s[:, 512 * half : 512 * (half + 1)],
-                in_=live["w2g"][:, 2048 * half : 2048 * (half + 1)],
+                in_=live["w2g", half][:],
             )
 
         def flip_h1(g, share):
@@ -142,11 +146,11 @@ def tile_gcnlayer_pa_kernel(tc, h1, adj, W2, b2, out):
                 in_=live["h1g", g][:],
             )
 
-        def project(g, nb):
-            if nb == 0:
-                live["hg", g] = wide.tile([P, 4 * OUT_F], BF16, tag="wide", name="hg", align_bytes=64)
-            hg = live["hg", g]
+        def project(b):
+            nh, g, q = blocks[b]
+            nb = 4 * nh + q
             acc = ps_a.tile([P, 4, P], F32, tag="acc", name="acc1")
+            live["prj", b] = acc
             for t in range(4):
                 x = 4 * g + t
                 nc.tensor.matmul_mx(
@@ -158,18 +162,25 @@ def tile_gcnlayer_pa_kernel(tc, h1, adj, W2, b2, out):
                     start=True,
                     stop=True,
                 )
+
+        def add_bias(b):
+            nh, g, q = blocks[b]
+            nb = 4 * nh + q
+            if q == 0:
+                live["hg", nh, g] = wide.tile([P, 4 * 512], BF16, tag="wide", name="hg", align_bytes=64)
             nc.vector.tensor_tensor(
-                out=hg[:, 512 * nb : 512 * (nb + 1)].rearrange("p (n t) -> p n t", t=4),
-                in0=acc[:].rearrange("p t n -> p n t"),
+                out=live["hg", nh, g][:, 512 * q : 512 * (q + 1)].rearrange("p (n t) -> p n t", t=4),
+                in0=live["prj", b][:].rearrange("p t n -> p n t"),
                 in1=bias[:, nb * P : (nb + 1) * P].unsqueeze(2).to_broadcast([P, P, 4]),
                 op=ALU.add,
             )
 
-        def quant_h(g):
+        def quant_h(nh, g):
+            col = OUT_F * g + 512 * nh
             nc.vector.quantize_mx(
-                out=hc[:, OUT_F * g : OUT_F * (g + 1)].bitcast(FP8X4),
-                scales=hs[:, OUT_F * g : OUT_F * (g + 1)],
-                in_=live["hg", g][:],
+                out=hc[:, col : col + 512].bitcast(FP8X4),
+                scales=hs[:, col : col + 512],
+                in_=live["hg", nh, g][:],
             )
 
         def inverse_root(x):
@@ -200,8 +211,10 @@ def tile_gcnlayer_pa_kernel(tc, h1, adj, W2, b2, out):
             if x > 0:
                 inverse_root(x - 1)
             nc.scalar.activation(
-                out=junk[:, 0:FOLD_W], in_=fold[:], func=ACT.Copy, accum_out=deg_p[:, x : x + 1]
+                out=junk2[:], in_=fold[:], func=ACT.Copy, accum_out=deg_p[:, x : x + 1]
             )
+
+        def add_loops(x):
             nc.gpsimd.tensor_tensor(
                 out=adj_i[:, x, :], in0=adj_sb[:, x, x * P : (x + 1) * P], in1=ident[:], op=ALU.add
             )
@@ -260,83 +273,96 @@ def tile_gcnlayer_pa_kernel(tc, h1, adj, W2, b2, out):
             live["asc", x] = asc
             nc.vector.quantize_mx(out=ac[:].bitcast(FP8X4), scales=asc[:], in_=live["ag", x][:])
 
-        def propagate(x):
+        def propagate(x, nh):
             ac = live["ac", x]
             asc = live["asc", x]
-            for nh in range(2):
-                acc = ps_a.tile([P, 512], F32, tag="acc", name="acc2")
-                live["acc", x, nh] = acc
-                for g in range(NG):
-                    col = OUT_F * g + 512 * nh
-                    nc.tensor.matmul_mx(
-                        out=acc[:],
-                        lhsT=ac[:, g * P : (g + 1) * P].bitcast(FP8X4),
-                        lhsT_scale=asc[:, g * P : (g + 1) * P],
-                        rhs=hc[:, col : col + 512].bitcast(FP8X4),
-                        rhs_scale=hs[:, col : col + 512],
-                        start=(g == 0),
-                        stop=(g == NG - 1),
-                    )
+            acc = ps_a.tile([P, 512], F32, tag="acc", name="acc2")
+            live["acc", x, nh] = acc
+            for g in range(NG):
+                col = OUT_F * g + 512 * nh
+                nc.tensor.matmul_mx(
+                    out=acc[:],
+                    lhsT=ac[:, g * P : (g + 1) * P].bitcast(FP8X4),
+                    lhsT_scale=asc[:, g * P : (g + 1) * P],
+                    rhs=hc[:, col : col + 512].bitcast(FP8X4),
+                    rhs_scale=hs[:, col : col + 512],
+                    start=(g == 0),
+                    stop=(g == NG - 1),
+                )
 
-        def store(x, in_halves):
-            ot = opool.tile([P, OUT_F], F32, tag="ot", name="ot")
-            for nh in range(2):
-                cols = slice(512 * nh, 512 * (nh + 1))
-                nc.scalar.copy(out=ot[:, cols], in_=live["acc", x, nh][:])
-                if in_halves:
-                    nc.sync.dma_start(out=out[x * P : (x + 1) * P, cols], in_=ot[:, cols])
-            if not in_halves:
-                nc.sync.dma_start(out=out[x * P : (x + 1) * P, :], in_=ot[:])
+        def drain(x, nh):
+            if nh == 0:
+                live["ot", x] = opool.tile([P, OUT_F], F32, tag="ot", name="ot")
+            cols = slice(512 * nh, 512 * (nh + 1))
+            nc.scalar.copy(out=live["ot", x][:, cols], in_=live["acc", x, nh][:])
+
+        def store(x):
+            nc.sync.dma_start(out=out[x * P : (x + 1) * P, :], in_=live["ot", x][:])
+
+        def store_half(x, nh):
+            cols = slice(512 * nh, 512 * (nh + 1))
+            nc.sync.dma_start(out=out[x * P : (x + 1) * P, cols], in_=live["ot", x][:, cols])
+
+        blocks = [(nh, g, q) for nh in range(2) for g in range(NG) for q in range(4)]
+        sums_after = {}
+        for x in range(NT):
+            sums_after.setdefault(max(-1, (40 + 17 * x) // 10), []).append(x)
+
+        def sums(b):
+            for x in sums_after.get(b, []):
+                row_sums(x)
+                add_loops(x)
+                if x % 4 == 0 and x > 0:
+                    spread(x // 4 - 1)
+
+        def step(b):
+            nh, g, q = blocks[b]
+            if b in {2: 2, 5: 3}:
+                flip_h1({2: 2, 5: 3}[b], False)
+            if nh == 0 and q == 2 and g < NG - 1:
+                quant_h1(g + 1)
+            if b == 10:
+                flip_w2(1, False)
+            if b == 12:
+                quant_w2(1)
+            if b + 2 < 32:
+                project(b + 2)
+            add_bias(b)
+            sums(b)
+            if q == 1 and b > 1:
+                quant_h(blocks[b - 2][0], blocks[b - 2][1])
 
         flip_h1(0, True)
         flip_w2(0, True)
         spread_bias()
+        for g in [1]:
+            flip_h1(g, False)
         quant_h1(0)
         quant_w2(0)
-        sums_after = {}
-        for x in range(NT):
-            b = min(31, (50 + 17 * x + 5) // 10)
-            sums_after[b] = sums_after.get(b, []) + [x]
-        spread_at = {}
+        sums(-1)
+        project(0)
+        project(1)
         for b in range(32):
-            g = b // 8
-            nb = b % 8
-            if b == 0:
-                flip_w2(1, False)
-            if b == 2:
-                quant_w2(1)
-            if nb == 3 and g < NG - 1:
-                flip_h1(g + 1, False)
-            if nb == 6 and g < NG - 1:
-                quant_h1(g + 1)
-            project(g, nb)
-            if nb == 0 and g > 0:
-                quant_h(g - 1)
-            for x in sums_after.get(b, []):
-                row_sums(x)
-                if x % 4 == 0 and x > 0:
-                    spread_at[b + 1] = x // 4 - 1
-            if b in spread_at:
-                spread(spread_at[b])
+            step(b)
         inverse_root(NT - 1)
         spread(NG - 1)
+        quant_h(1, NG - 1)
         scale(0)
         flip_adj(0)
         regroup(0)
-        quant_h(NG - 1)
-        scale(1)
-        flip_adj(1)
-        quant_adj(0)
-        regroup(1)
-        for x in range(NT):
-            propagate(x)
-            if x + 2 < NT:
-                scale(x + 2)
-                flip_adj(x + 2)
-            if x + 1 < NT:
-                quant_adj(x + 1)
-            if x > 0:
-                store(x - 1, False)
-            if x + 2 < NT:
-                regroup(x + 2)
-        store(NT - 1, True)
+        for x in range(1, NT + 1):
+            if x < NT:
+                scale(x)
+            quant_adj(x - 1)
+            if x < NT:
+                flip_adj(x)
+            for nh in range(2):
+                propagate(x - 1, nh)
+            if x < NT:
+                regroup(x)
+            for nh in range(2):
+                drain(x - 1, nh)
+                if x == NT:
+                    store_half(x - 1, nh)
+            if x < NT:
+                store(x - 1)

@@ -62,14 +62,12 @@ def tile_gcnlayer_pa_kernel(tc, h1, adj, W2, b2, out):
         adj_i = keep.tile([P, NT, P], F32)
         live = {}
 
-        nc.vector.memset(warm[:], 1.0)
         nc.vector.memset(b_row[:], 0.0)
+        nc.vector.memset(warm[:], 1.0)
         nc.vector.memset(ones_b[:], 1.0)
         nc.scalar.activation(out=warm2[:], in_=warm[:], func=ACT.Abs_reciprocal_sqrt)
         make_identity(nc, ident[:])
         make_identity(nc, ident_b[:])
-
-        nc.scalar.dma_start(out=b_row[0:1, :], in_=b2.unsqueeze(0))
 
         def load_h1(g):
             nc.sync.dma_start(
@@ -87,6 +85,7 @@ def tile_gcnlayer_pa_kernel(tc, h1, adj, W2, b2, out):
             nc.sync.dma_start(out=adj_sb[:, x, :], in_=adj[x * P : (x + 1) * P, :])
 
         load_h1(0)
+        nc.sync.dma_start(out=b_row[0:1, :], in_=b2.unsqueeze(0))
         load_w2(0)
         for g in range(1, NG):
             load_h1(g)
@@ -238,33 +237,33 @@ def tile_gcnlayer_pa_kernel(tc, h1, adj, W2, b2, out):
                 op1=ALU.mult,
             )
 
-        def scale(x):
-            live["scaled", x] = spool.tile([P, N_NODES], BF16, tag="scaled", name="scaled", align_bytes=64)
-            d0 = x * P
-            d1 = d0 + P
-            if x > 0:
-                scale_piece(x, 0, d0, adj_sb[:, x, 0:d0])
-            scale_piece(x, d0, d1, adj_i[:, x, :])
-            if x < NT - 1:
-                scale_piece(x, d1, N_NODES, adj_sb[:, x, d1:N_NODES])
+        def scale(x, lo, hi):
+            if lo == 0:
+                live["scaled", x] = spool.tile([P, N_NODES], BF16, tag="scaled", name="scaled", align_bytes=64)
+            d0 = max(lo, min(hi, x * P))
+            d1 = max(lo, min(hi, (x + 1) * P))
+            if d0 > lo:
+                scale_piece(x, lo, d0, adj_sb[:, x, lo:d0])
+            if d1 > d0:
+                scale_piece(x, d0, d1, adj_i[:, x, :])
+            if hi > d1:
+                scale_piece(x, d1, hi, adj_sb[:, x, d1:hi])
 
-        def flip_adj(x):
+        def flip_adj(x, b):
             words = live["scaled", x][:].bitcast(F32)
-            for b in range(2):
-                tp = ps_t.tile([P, 4, P], F32, tag="tp", name="tpa")
-                live["tp", x, b] = tp
-                for c in range(4):
-                    col = (4 * b + c) * P
-                    nc.tensor.transpose(tp[:, c, :], words[:, col : col + P], ident[:])
+            tp = ps_t.tile([P, 4, P], F32, tag="tp", name="tpa")
+            live["tp", x, b] = tp
+            for c in range(4):
+                col = (4 * b + c) * P
+                nc.tensor.transpose(tp[:, c, :], words[:, col : col + P], ident[:])
 
-        def regroup(x):
-            ag = grp.tile([P, 4 * 512], BF16, tag="grp", name="ag", align_bytes=64)
-            live["ag", x] = ag
-            for b in range(2):
-                nc.scalar.copy(
-                    out=ag[:].bitcast(F32)[:, 512 * b : 512 * (b + 1)].rearrange("p (g i u) -> p g i u", g=2, u=2),
-                    in_=live["tp", x, b][:].rearrange("p (g u) i -> p g i u", g=2),
-                )
+        def regroup(x, b):
+            if b == 0:
+                live["ag", x] = grp.tile([P, 4 * 512], BF16, tag="grp", name="ag", align_bytes=64)
+            nc.scalar.copy(
+                out=live["ag", x][:].bitcast(F32)[:, 512 * b : 512 * (b + 1)].rearrange("p (g i u) -> p g i u", g=2, u=2),
+                in_=live["tp", x, b][:].rearrange("p (g u) i -> p g i u", g=2),
+            )
 
         def quant_adj(x):
             ac = cpool.tile([P, 512], U32, tag="ac", name="ac", align_bytes=64)
@@ -346,20 +345,37 @@ def tile_gcnlayer_pa_kernel(tc, h1, adj, W2, b2, out):
             step(b)
         inverse_root(NT - 1)
         spread(NG - 1)
+        scale(0, 0, 1024)
+        flip_adj(0, 0)
+        regroup(0, 0)
+        scale(0, 1024, 1536)
         quant_h(1, NG - 1)
-        scale(0)
-        flip_adj(0)
-        regroup(0)
+        scale(0, 1536, N_NODES)
+        flip_adj(0, 1)
+        regroup(0, 1)
         for x in range(1, NT + 1):
-            if x < NT:
-                scale(x)
-            quant_adj(x - 1)
-            if x < NT:
-                flip_adj(x)
-            for nh in range(2):
-                propagate(x - 1, nh)
-            if x < NT:
-                regroup(x)
+            if x == 1:
+                scale(1, 0, 1024)
+                quant_adj(0)
+                flip_adj(1, 0)
+                scale(1, 1024, N_NODES)
+                propagate(0, 0)
+                propagate(0, 1)
+                flip_adj(1, 1)
+                regroup(1, 0)
+                regroup(1, 1)
+            else:
+                if x < NT:
+                    scale(x, 0, N_NODES)
+                quant_adj(x - 1)
+                if x < NT:
+                    flip_adj(x, 0)
+                    flip_adj(x, 1)
+                propagate(x - 1, 0)
+                propagate(x - 1, 1)
+                if x < NT:
+                    regroup(x, 0)
+                    regroup(x, 1)
             for nh in range(2):
                 drain(x - 1, nh)
                 if x == NT:

@@ -18,7 +18,7 @@ OUT_F = 1024
 NT = N_NODES // P
 NG = NT // 4
 FOLD_W = 128
-N_FOLD = 11
+N_FOLD = 10
 FOLDED = FOLD_W * N_FOLD
 
 FLOPS = 2 * N_NODES * HID * OUT_F + 2 * N_NODES * N_NODES * OUT_F
@@ -45,7 +45,7 @@ def tile_gcnlayer_pa_kernel(tc, h1, adj, W2, b2, out):
         h1n = keep.tile([P, NT * HID], BF16)
         bias = keep.tile([P, OUT_F], F32)
         b_row = keep.tile([P, OUT_F], BF16)
-        ones_b = keep.tile([P, P], BF16)
+        ones_w = keep.tile([P, 512], BF16)
         adj_sb = keep.tile([P, NT, N_NODES], BF16)
         w2c = keep.tile([P, OUT_F], U32, align_bytes=64)
         w2s = keep.tile([P, OUT_F], U8, align_bytes=64)
@@ -62,45 +62,49 @@ def tile_gcnlayer_pa_kernel(tc, h1, adj, W2, b2, out):
         adj_i = keep.tile([P, NT, P], F32)
         live = {}
 
+        nc.vector.memset(ones_w[:], 1.0)
         nc.vector.memset(b_row[:], 0.0)
         nc.vector.memset(warm[:], 1.0)
-        nc.vector.memset(ones_b[:], 1.0)
         nc.scalar.activation(out=warm2[:], in_=warm[:], func=ACT.Abs_reciprocal_sqrt)
         make_identity(nc, ident[:])
         make_identity(nc, ident_b[:])
 
-        def load_h1(g):
-            nc.sync.dma_start(
-                out=h1n[:, 4 * g * HID : 4 * (g + 1) * HID].rearrange("p (u e k) -> p u e k", u=2, e=2),
-                in_=h1[4 * g * P : 4 * (g + 1) * P, :].rearrange("(u p e) k -> p u e k", p=P, e=2),
-            )
+        def load_h1(g, halves):
+            dst = h1n[:, 4 * g * HID : 4 * (g + 1) * HID].rearrange("p (u e k) -> p u e k", u=2, e=2)
+            src = h1[4 * g * P : 4 * (g + 1) * P, :].rearrange("(u p e) k -> p u e k", p=P, e=2)
+            for us in [slice(0, 1), slice(1, 2)] if halves else [slice(0, 2)]:
+                nc.sync.dma_start(out=dst[:, us], in_=src[:, us])
 
-        def load_w2(half):
+        def load_w2(first, count):
             nc.sync.dma_start(
-                out=w2n[:, 4 * half * HID : 4 * (half + 1) * HID].rearrange("p (c k) -> p c k", k=HID),
-                in_=W2[4 * half * P : 4 * (half + 1) * P, :].rearrange("(c p) k -> p c k", p=P),
+                out=w2n[:, first * HID : (first + count) * HID].rearrange("p (c k) -> p c k", k=HID),
+                in_=W2[first * P : (first + count) * P, :].rearrange("(c p) k -> p c k", p=P),
             )
 
         def load_adj(x):
             nc.sync.dma_start(out=adj_sb[:, x, :], in_=adj[x * P : (x + 1) * P, :])
 
-        load_h1(0)
+        load_h1(0, True)
         nc.sync.dma_start(out=b_row[0:1, :], in_=b2.unsqueeze(0))
-        load_w2(0)
+        load_w2(0, 2)
+        load_w2(2, 2)
         for g in range(1, NG):
-            load_h1(g)
+            load_h1(g, False)
         for x in range(NT):
             load_adj(x)
-            if x == 6:
-                load_w2(1)
+            if x == 3:
+                load_w2(4, 4)
 
-        def spread_bias():
-            for nh in range(2):
-                pb = ps_a.tile([P, 512], F32, tag="acc", name="pb")
-                nc.tensor.matmul(
-                    out=pb[:], lhsT=ones_b[:], rhs=b_row[:, 512 * nh : 512 * (nh + 1)], start=True, stop=True
-                )
-                nc.scalar.copy(out=bias[:, 512 * nh : 512 * (nh + 1)], in_=pb[:])
+        def warm_up():
+            pw = ps_a.tile([P, 512], F32, tag="acc", name="pw")
+            for c in range(6):
+                nc.tensor.matmul(out=pw[:], lhsT=ones_w[:, 0:P], rhs=ones_w[:], start=True, stop=True)
+
+        def spread_bias(nh):
+            pb = ps_a.tile([P, 512], F32, tag="acc", name="pb")
+            cols = slice(512 * nh, 512 * (nh + 1))
+            nc.tensor.matmul(out=pb[:], lhsT=ones_w[:, 0:P], rhs=b_row[:, cols], start=True, stop=True)
+            nc.scalar.copy(out=bias[:, cols], in_=pb[:])
 
         def flip_rows(src_words, first_tile, dst_words, on_vector):
             tp = ps_t.tile([P, 4, P], F32, tag="tp", name="tp")
@@ -115,20 +119,14 @@ def tile_gcnlayer_pa_kernel(tc, h1, adj, W2, b2, out):
             else:
                 nc.scalar.copy(out=dst, in_=src)
 
-        def flip_w2(half, share):
-            w2g = wide.tile([P, 4 * 512], BF16, tag="wide", name="w2g", align_bytes=64)
-            live["w2g", half] = w2g
-            for b in range(2):
-                flip_rows(
-                    w2n[:].bitcast(F32), 4 * half + 2 * b, w2g[:].bitcast(F32)[:, 512 * b : 512 * (b + 1)], share and b == 1
-                )
+        def flip_w2(pair):
+            w2g = wide.tile([P, 4 * 256], BF16, tag="w2g", name="w2g", align_bytes=64)
+            live["w2g", pair] = w2g
+            flip_rows(w2n[:].bitcast(F32), 2 * pair, w2g[:].bitcast(F32), False)
 
-        def quant_w2(half):
-            nc.vector.quantize_mx(
-                out=w2c[:, 512 * half : 512 * (half + 1)].bitcast(FP8X4),
-                scales=w2s[:, 512 * half : 512 * (half + 1)],
-                in_=live["w2g", half][:],
-            )
+        def quant_w2(pair):
+            cols = slice(256 * pair, 256 * (pair + 1))
+            nc.vector.quantize_mx(out=w2c[:, cols].bitcast(FP8X4), scales=w2s[:, cols], in_=live["w2g", pair][:])
 
         def flip_h1(g, share):
             h1g = grp.tile([P, 4 * 512], BF16, tag="grp", name="h1g", align_bytes=64)
@@ -272,35 +270,30 @@ def tile_gcnlayer_pa_kernel(tc, h1, adj, W2, b2, out):
             live["asc", x] = asc
             nc.vector.quantize_mx(out=ac[:].bitcast(FP8X4), scales=asc[:], in_=live["ag", x][:])
 
-        def propagate(x, nh):
+        def propagate(x, lo, hi):
             ac = live["ac", x]
             asc = live["asc", x]
-            acc = ps_a.tile([P, 512], F32, tag="acc", name="acc2")
-            live["acc", x, nh] = acc
+            acc = ps_a.tile([P, hi - lo], F32, tag="acc", name="acc2")
+            live["acc", x, lo] = acc
             for g in range(NG):
-                col = OUT_F * g + 512 * nh
+                cols = slice(OUT_F * g + lo, OUT_F * g + hi)
                 nc.tensor.matmul_mx(
                     out=acc[:],
                     lhsT=ac[:, g * P : (g + 1) * P].bitcast(FP8X4),
                     lhsT_scale=asc[:, g * P : (g + 1) * P],
-                    rhs=hc[:, col : col + 512].bitcast(FP8X4),
-                    rhs_scale=hs[:, col : col + 512],
+                    rhs=hc[:, cols].bitcast(FP8X4),
+                    rhs_scale=hs[:, cols],
                     start=(g == 0),
                     stop=(g == NG - 1),
                 )
 
-        def drain(x, nh):
-            if nh == 0:
+        def drain(x, lo, hi):
+            if lo == 0:
                 live["ot", x] = opool.tile([P, OUT_F], F32, tag="ot", name="ot")
-            cols = slice(512 * nh, 512 * (nh + 1))
-            nc.scalar.copy(out=live["ot", x][:, cols], in_=live["acc", x, nh][:])
+            nc.scalar.copy(out=live["ot", x][:, lo:hi], in_=live["acc", x, lo][:])
 
-        def store(x):
-            nc.sync.dma_start(out=out[x * P : (x + 1) * P, :], in_=live["ot", x][:])
-
-        def store_half(x, nh):
-            cols = slice(512 * nh, 512 * (nh + 1))
-            nc.sync.dma_start(out=out[x * P : (x + 1) * P, cols], in_=live["ot", x][:, cols])
+        def store(x, lo, hi):
+            nc.sync.dma_start(out=out[x * P : (x + 1) * P, lo:hi], in_=live["ot", x][:, lo:hi])
 
         blocks = [(nh, g, q) for nh in range(2) for g in range(NG) for q in range(4)]
         sums_after = {}
@@ -316,69 +309,75 @@ def tile_gcnlayer_pa_kernel(tc, h1, adj, W2, b2, out):
 
         def step(b):
             nh, g, q = blocks[b]
-            if b in {2: 2, 5: 3}:
-                flip_h1({2: 2, 5: 3}[b], False)
+            if b in {1: 2, 4: 3}:
+                flip_h1({1: 2, 4: 3}[b], False)
             if nh == 0 and q == 2 and g < NG - 1:
                 quant_h1(g + 1)
             if b == 10:
-                flip_w2(1, False)
-            if b == 12:
+                flip_w2(2)
+                spread_bias(1)
+            if b == 10 + 2:
+                flip_w2(3)
+                quant_w2(2)
+            if b == 10 + 4:
+                quant_w2(3)
+            if b == 0:
+                add_bias(0)
                 quant_w2(1)
-            if b + 2 < 32:
-                project(b + 2)
-            add_bias(b)
+                project(2)
+            else:
+                if b + 2 < 32:
+                    project(b + 2)
+                add_bias(b)
             sums(b)
             if q == 1 and b > 1:
                 quant_h(blocks[b - 2][0], blocks[b - 2][1])
+            if b in {26: 0, 29: 1}:
+                scale({26: 0, 29: 1}[b], 0, 1024)
 
+        warm_up()
         flip_h1(0, True)
-        flip_w2(0, True)
-        spread_bias()
-        for g in [1]:
-            flip_h1(g, False)
+        flip_w2(0)
+        spread_bias(0)
         quant_h1(0)
         quant_w2(0)
-        sums(-1)
+        flip_w2(1)
         project(0)
         project(1)
+        for g in [1]:
+            flip_h1(g, False)
+        sums(-1)
         for b in range(32):
             step(b)
         inverse_root(NT - 1)
+        early = len({26: 0, 29: 1})
+        for x in range(early):
+            flip_adj(x, 0)
+            regroup(x, 0)
         spread(NG - 1)
-        scale(0, 0, 1024)
-        flip_adj(0, 0)
-        regroup(0, 0)
         scale(0, 1024, 1536)
         quant_h(1, NG - 1)
         scale(0, 1536, N_NODES)
         flip_adj(0, 1)
         regroup(0, 1)
         for x in range(1, NT + 1):
-            if x == 1:
-                scale(1, 0, 1024)
-                quant_adj(0)
-                flip_adj(1, 0)
-                scale(1, 1024, N_NODES)
-                propagate(0, 0)
-                propagate(0, 1)
-                flip_adj(1, 1)
-                regroup(1, 0)
-                regroup(1, 1)
-            else:
-                if x < NT:
-                    scale(x, 0, N_NODES)
-                quant_adj(x - 1)
-                if x < NT:
-                    flip_adj(x, 0)
-                    flip_adj(x, 1)
-                propagate(x - 1, 0)
-                propagate(x - 1, 1)
-                if x < NT:
-                    regroup(x, 0)
-                    regroup(x, 1)
-            for nh in range(2):
-                drain(x - 1, nh)
-                if x == NT:
-                    store_half(x - 1, nh)
             if x < NT:
-                store(x - 1)
+                scale(x, 1024 if x < early else 0, N_NODES)
+            quant_adj(x - 1)
+            if x < NT:
+                if x >= early:
+                    flip_adj(x, 0)
+                flip_adj(x, 1)
+            parts = [(0, 512), (512, 1024)] if x < NT else [(0, 512), (512, 768), (768, 1024)]
+            for lo, hi in parts:
+                propagate(x - 1, lo, hi)
+            if x < NT:
+                if x >= early:
+                    regroup(x, 0)
+                regroup(x, 1)
+            for lo, hi in parts:
+                drain(x - 1, lo, hi)
+                if x == NT:
+                    store(x - 1, lo, hi)
+            if x < NT:
+                store(x - 1, 0, OUT_F)

@@ -47,12 +47,12 @@ def tile_gcnlayer_pa_kernel(tc, h1, adj, W2, b2, out):
         b_row = keep.tile([P, OUT_F], BF16)
         ones_w = keep.tile([P, 512], BF16)
         adj_sb = keep.tile([P, NT, N_NODES], BF16)
-        w2c = keep.tile([P, OUT_F], U32, align_bytes=64)
-        w2s = keep.tile([P, OUT_F], U8, align_bytes=64)
-        h1c = keep.tile([P, N_NODES], U32, align_bytes=64)
-        h1s = keep.tile([P, N_NODES], U8, align_bytes=64)
-        hc = keep.tile([P, NG * OUT_F], U32, align_bytes=64)
-        hs = keep.tile([P, NG * OUT_F], U8, align_bytes=64)
+        w2c = keep.tile([P, OUT_F], U32, align_bytes=256)
+        w2s = keep.tile([P, OUT_F], U8, align_bytes=256)
+        h1c = keep.tile([P, N_NODES], U32, align_bytes=256)
+        h1s = keep.tile([P, N_NODES], U8, align_bytes=256)
+        hc = keep.tile([P, NG * OUT_F], U32, align_bytes=256)
+        hs = keep.tile([P, NG * OUT_F], U8, align_bytes=256)
         deg_p = keep.tile([P, NT], F32)
         deg_s = keep.tile([P, NT], F32)
         r = keep.tile([P, NT], F32)
@@ -119,10 +119,10 @@ def tile_gcnlayer_pa_kernel(tc, h1, adj, W2, b2, out):
             else:
                 nc.scalar.copy(out=dst, in_=src)
 
-        def flip_w2(pair):
+        def flip_w2(pair, on_vector):
             w2g = wide.tile([P, 4 * 256], BF16, tag="w2g", name="w2g", align_bytes=64)
             live["w2g", pair] = w2g
-            flip_rows(w2n[:].bitcast(F32), 2 * pair, w2g[:].bitcast(F32), False)
+            flip_rows(w2n[:].bitcast(F32), 2 * pair, w2g[:].bitcast(F32), on_vector)
 
         def quant_w2(pair):
             cols = slice(256 * pair, 256 * (pair + 1))
@@ -264,8 +264,8 @@ def tile_gcnlayer_pa_kernel(tc, h1, adj, W2, b2, out):
             )
 
         def quant_adj(x):
-            ac = cpool.tile([P, 512], U32, tag="ac", name="ac", align_bytes=64)
-            asc = cpool.tile([P, 512], U8, tag="asc", name="asc", align_bytes=64)
+            ac = cpool.tile([P, 512], U32, tag="ac", name="ac", align_bytes=256)
+            asc = cpool.tile([P, 512], U8, tag="asc", name="asc", align_bytes=256)
             live["ac", x] = ac
             live["asc", x] = asc
             nc.vector.quantize_mx(out=ac[:].bitcast(FP8X4), scales=asc[:], in_=live["ag", x][:])
@@ -304,22 +304,22 @@ def tile_gcnlayer_pa_kernel(tc, h1, adj, W2, b2, out):
             for x in sums_after.get(b, []):
                 row_sums(x)
                 add_loops(x)
+                if x == 4:
+                    flip_w2(2, False)
+                    flip_w2(3, False)
+                    spread_bias(1)
                 if x % 4 == 0 and x > 0:
                     spread(x // 4 - 1)
 
         def step(b):
             nh, g, q = blocks[b]
-            if b in {1: 2, 4: 3}:
-                flip_h1({1: 2, 4: 3}[b], False)
+            for gf in {2: [2, 3]}.get(b, []):
+                flip_h1(gf, False)
             if nh == 0 and q == 2 and g < NG - 1:
                 quant_h1(g + 1)
-            if b == 10:
-                flip_w2(2)
-                spread_bias(1)
-            if b == 10 + 2:
-                flip_w2(3)
+            if b == 13:
                 quant_w2(2)
-            if b == 10 + 4:
+            if b == 15:
                 quant_w2(3)
             if b == 0:
                 add_bias(0)
@@ -332,16 +332,16 @@ def tile_gcnlayer_pa_kernel(tc, h1, adj, W2, b2, out):
             sums(b)
             if q == 1 and b > 1:
                 quant_h(blocks[b - 2][0], blocks[b - 2][1])
-            if b in {26: 0, 29: 1}:
-                scale({26: 0, 29: 1}[b], 0, 1024)
+            if b in {24: 0, 28: 1}:
+                scale({24: 0, 28: 1}[b], 0, 1024)
 
         warm_up()
         flip_h1(0, True)
-        flip_w2(0)
+        flip_w2(0, False)
         spread_bias(0)
         quant_h1(0)
         quant_w2(0)
-        flip_w2(1)
+        flip_w2(1, False)
         project(0)
         project(1)
         for g in [1]:
@@ -350,7 +350,7 @@ def tile_gcnlayer_pa_kernel(tc, h1, adj, W2, b2, out):
         for b in range(32):
             step(b)
         inverse_root(NT - 1)
-        early = len({26: 0, 29: 1})
+        early = len({24: 0, 28: 1})
         for x in range(early):
             flip_adj(x, 0)
             regroup(x, 0)

@@ -30,8 +30,8 @@ def tile_gcnlayer_pa_kernel(tc, h1, adj, W2, b2, out):
         keep = ctx.enter_context(tc.tile_pool(name="keep", bufs=1))
         wide = ctx.enter_context(tc.tile_pool(name="wide", bufs=3))
         grp = ctx.enter_context(tc.tile_pool(name="grp", bufs=4))
-        spool = ctx.enter_context(tc.tile_pool(name="spool", bufs=3))
-        cpool = ctx.enter_context(tc.tile_pool(name="cpool", bufs=3))
+        spool = ctx.enter_context(tc.tile_pool(name="spool", bufs=5))
+        cpool = ctx.enter_context(tc.tile_pool(name="cpool", bufs=4))
         opool = ctx.enter_context(tc.tile_pool(name="opool", bufs=3))
         ps_t = ctx.enter_context(tc.psum_pool(name="ps_t", bufs=4))
         ps_a = ctx.enter_context(tc.psum_pool(name="ps_a", bufs=4))
@@ -263,24 +263,25 @@ def tile_gcnlayer_pa_kernel(tc, h1, adj, W2, b2, out):
                 in_=live["tp", x, b][:].rearrange("p (g u) i -> p g i u", g=2),
             )
 
-        def quant_adj(x):
-            ac = cpool.tile([P, 512], U32, tag="ac", name="ac", align_bytes=256)
-            asc = cpool.tile([P, 512], U8, tag="asc", name="asc", align_bytes=256)
-            live["ac", x] = ac
-            live["asc", x] = asc
-            nc.vector.quantize_mx(out=ac[:].bitcast(FP8X4), scales=asc[:], in_=live["ag", x][:])
+        def quant_adj(x, lo, hi):
+            if lo == 0:
+                live["ac", x] = cpool.tile([P, 512], U32, tag="ac", name="ac", align_bytes=256)
+                live["asc", x] = cpool.tile([P, 512], U8, tag="asc", name="asc", align_bytes=256)
+            nc.vector.quantize_mx(
+                out=live["ac", x][:, lo // 4 : hi // 4].bitcast(FP8X4),
+                scales=live["asc", x][:, lo // 4 : hi // 4],
+                in_=live["ag", x][:, lo:hi],
+            )
 
-        def propagate(x, lo, hi):
-            ac = live["ac", x]
-            asc = live["asc", x]
-            acc = ps_a.tile([P, hi - lo], F32, tag="acc", name="acc2")
-            live["acc", x, lo] = acc
-            for g in range(NG):
+        def propagate(x, lo, hi, passes):
+            if passes[0] == 0:
+                live["acc", x, lo] = ps_a.tile([P, hi - lo], F32, tag="acc", name="acc2")
+            for g in passes:
                 cols = slice(OUT_F * g + lo, OUT_F * g + hi)
                 nc.tensor.matmul_mx(
-                    out=acc[:],
-                    lhsT=ac[:, g * P : (g + 1) * P].bitcast(FP8X4),
-                    lhsT_scale=asc[:, g * P : (g + 1) * P],
+                    out=live["acc", x, lo][:],
+                    lhsT=live["ac", x][:, g * P : (g + 1) * P].bitcast(FP8X4),
+                    lhsT_scale=live["asc", x][:, g * P : (g + 1) * P],
                     rhs=hc[:, cols].bitcast(FP8X4),
                     rhs_scale=hs[:, cols],
                     start=(g == 0),
@@ -298,7 +299,7 @@ def tile_gcnlayer_pa_kernel(tc, h1, adj, W2, b2, out):
         blocks = [(nh, g, q) for nh in range(2) for g in range(NG) for q in range(4)]
         sums_after = {}
         for x in range(NT):
-            sums_after.setdefault(max(-1, (40 + 17 * x) // 10), []).append(x)
+            sums_after.setdefault(max(-1, (30 + 17 * x) // 10), []).append(x)
 
         def sums(b):
             for x in sums_after.get(b, []):
@@ -308,8 +309,13 @@ def tile_gcnlayer_pa_kernel(tc, h1, adj, W2, b2, out):
                     flip_w2(2, False)
                     flip_w2(3, False)
                     spread_bias(1)
+                if x in {12: 0, 15: 1}:
+                    flip_adj({12: 0, 15: 1}[x], 0)
+                    regroup({12: 0, 15: 1}[x], 0)
                 if x % 4 == 0 and x > 0:
                     spread(x // 4 - 1)
+
+        done = {}
 
         def step(b):
             nh, g, q = blocks[b]
@@ -332,8 +338,14 @@ def tile_gcnlayer_pa_kernel(tc, h1, adj, W2, b2, out):
             sums(b)
             if q == 1 and b > 1:
                 quant_h(blocks[b - 2][0], blocks[b - 2][1])
-            if b in {24: 0, 28: 1}:
-                scale({24: 0, 28: 1}[b], 0, 1024)
+            for x, lo, hi in {14:[(0,0,512)],16:[(1,0,512)],18:[(2,0,512)],20:[(3,0,512)],22:[(0,512,1024)],25:[(1,512,1024)]}.get(b, []):
+                scale(x, lo, hi)
+                done[x] = hi
+            if b in {}:
+                flip_adj({}[b], 0)
+                regroup({}[b], 0)
+            if b in {28: 0, 31: 1}:
+                quant_adj({28: 0, 31: 1}[b], 0, 1024)
 
         warm_up()
         flip_h1(0, True)
@@ -350,27 +362,33 @@ def tile_gcnlayer_pa_kernel(tc, h1, adj, W2, b2, out):
         for b in range(32):
             step(b)
         inverse_root(NT - 1)
-        early = len({24: 0, 28: 1})
-        for x in range(early):
+        early = len([x for x in done if done[x] >= 1024])
+        pre = len({28: 0, 31: 1})
+        for x in range(pre, early):
             flip_adj(x, 0)
             regroup(x, 0)
+        propagate(0, 0, 512, range(2))
+        propagate(0, 512, 1024, range(2))
         spread(NG - 1)
-        scale(0, 1024, 1536)
+        propagate(1, 0, 512, range(2))
+        propagate(1, 512, 1024, range(2))
+        if done[0] < 1536:
+            scale(0, done[0], 1536)
         quant_h(1, NG - 1)
         scale(0, 1536, N_NODES)
         flip_adj(0, 1)
         regroup(0, 1)
         for x in range(1, NT + 1):
             if x < NT:
-                scale(x, 1024 if x < early else 0, N_NODES)
-            quant_adj(x - 1)
+                scale(x, done.get(x, 0), N_NODES)
+            quant_adj(x - 1, 1024 if x - 1 < pre else 0, N_NODES)
             if x < NT:
                 if x >= early:
                     flip_adj(x, 0)
                 flip_adj(x, 1)
             parts = [(0, 512), (512, 1024)] if x < NT else [(0, 512), (512, 768), (768, 1024)]
             for lo, hi in parts:
-                propagate(x - 1, lo, hi)
+                propagate(x - 1, lo, hi, range(2 if x - 1 < pre else 0, NG))
             if x < NT:
                 if x >= early:
                     regroup(x, 0)

@@ -86,7 +86,8 @@ def tile_gcnlayer_pa_kernel(tc, h1, adj, W2, b2, out):
 
         load_h1(0, True)
         nc.sync.dma_start(out=b_row[0:1, :], in_=b2.unsqueeze(0))
-        load_w2(0, 2)
+        load_w2(0, 1)
+        load_w2(1, 1)
         load_w2(2, 2)
         for g in range(1, NG):
             load_h1(g, False)
@@ -100,40 +101,44 @@ def tile_gcnlayer_pa_kernel(tc, h1, adj, W2, b2, out):
             for c in range(6):
                 nc.tensor.matmul(out=pw[:], lhsT=ones_w[:, 0:P], rhs=ones_w[:], start=True, stop=True)
 
-        def spread_bias(nh):
+        def spread_bias(nh, on_vector):
             pb = ps_a.tile([P, 512], F32, tag="acc", name="pb")
             cols = slice(512 * nh, 512 * (nh + 1))
             nc.tensor.matmul(out=pb[:], lhsT=ones_w[:, 0:P], rhs=b_row[:, cols], start=True, stop=True)
-            nc.scalar.copy(out=bias[:, cols], in_=pb[:])
+            if on_vector:
+                nc.vector.tensor_copy(out=bias[:, cols], in_=pb[:])
+            else:
+                nc.scalar.copy(out=bias[:, cols], in_=pb[:])
 
-        def flip_rows(src_words, first_tile, dst_words, on_vector):
-            tp = ps_t.tile([P, 4, P], F32, tag="tp", name="tp")
-            for c in range(2):
+        def flip_rows(src_words, first_tile, count, dst_words, on_vector):
+            tp = ps_t.tile([P, 2 * count, P], F32, tag="tp", name="tp")
+            for c in range(count):
                 for u in range(2):
                     col = (first_tile + c) * (HID // 2) + u * P
                     nc.tensor.transpose(tp[:, 2 * c + u, :], src_words[:, col : col + P], ident[:])
-            dst = dst_words.rearrange("p (c n u) -> p c n u", c=2, u=2)
-            src = tp[:].rearrange("p (c u) n -> p c n u", c=2)
+            dst = dst_words.rearrange("p (c n u) -> p c n u", c=count, u=2)
+            src = tp[:].rearrange("p (c u) n -> p c n u", c=count)
             if on_vector:
                 nc.vector.tensor_copy(out=dst, in_=src)
             else:
                 nc.scalar.copy(out=dst, in_=src)
 
-        def flip_w2(pair, on_vector):
-            w2g = wide.tile([P, 4 * 256], BF16, tag="w2g", name="w2g", align_bytes=64)
-            live["w2g", pair] = w2g
-            flip_rows(w2n[:].bitcast(F32), 2 * pair, w2g[:].bitcast(F32), on_vector)
+        def flip_w2(first, count):
+            w2g_room = wide.tile([P, 2 * 512], BF16, tag="w2g", name="w2g", align_bytes=64)
+            w2g = w2g_room[:, 0 : 512 * count]
+            live["w2g", first] = w2g
+            flip_rows(w2n[:].bitcast(F32), first, count, w2g.bitcast(F32), False)
 
-        def quant_w2(pair):
-            cols = slice(256 * pair, 256 * (pair + 1))
-            nc.vector.quantize_mx(out=w2c[:, cols].bitcast(FP8X4), scales=w2s[:, cols], in_=live["w2g", pair][:])
+        def quant_w2(first, count):
+            cols = slice(P * first, P * (first + count))
+            nc.vector.quantize_mx(out=w2c[:, cols].bitcast(FP8X4), scales=w2s[:, cols], in_=live["w2g", first])
 
         def flip_h1(g, share):
             h1g = grp.tile([P, 4 * 512], BF16, tag="grp", name="h1g", align_bytes=64)
             live["h1g", g] = h1g
             for b in range(2):
                 flip_rows(
-                    h1n[:].bitcast(F32), 4 * g + 2 * b, h1g[:].bitcast(F32)[:, 512 * b : 512 * (b + 1)], share and b == 1
+                    h1n[:].bitcast(F32), 4 * g + 2 * b, 2, h1g[:].bitcast(F32)[:, 512 * b : 512 * (b + 1)], share and b == 1
                 )
 
         def quant_h1(g):
@@ -306,9 +311,9 @@ def tile_gcnlayer_pa_kernel(tc, h1, adj, W2, b2, out):
                 row_sums(x)
                 add_loops(x)
                 if x == 4:
-                    flip_w2(2, False)
-                    flip_w2(3, False)
-                    spread_bias(1)
+                    flip_w2(4, 2)
+                    flip_w2(6, 2)
+                    spread_bias(1, False)
                 if x in {12: 0, 15: 1}:
                     flip_adj({12: 0, 15: 1}[x], 0)
                     regroup({12: 0, 15: 1}[x], 0)
@@ -324,12 +329,14 @@ def tile_gcnlayer_pa_kernel(tc, h1, adj, W2, b2, out):
             if nh == 0 and q == 2 and g < NG - 1:
                 quant_h1(g + 1)
             if b == 13:
-                quant_w2(2)
+                quant_w2(4, 2)
             if b == 15:
-                quant_w2(3)
+                quant_w2(6, 2)
             if b == 0:
                 add_bias(0)
-                quant_w2(1)
+                quant_w2(1, 1)
+                project(1)
+                quant_w2(2, 2)
                 project(2)
             else:
                 if b + 2 < 32:
@@ -349,13 +356,13 @@ def tile_gcnlayer_pa_kernel(tc, h1, adj, W2, b2, out):
 
         warm_up()
         flip_h1(0, True)
-        flip_w2(0, False)
-        spread_bias(0)
+        flip_w2(0, 1)
         quant_h1(0)
-        quant_w2(0)
-        flip_w2(1, False)
+        quant_w2(0, 1)
+        spread_bias(0, True)
+        flip_w2(1, 1)
+        flip_w2(2, 2)
         project(0)
-        project(1)
         for g in [1]:
             flip_h1(g, False)
         sums(-1)

@@ -93,7 +93,7 @@ def tile_gcnlayer_pa_kernel(tc, h1, adj, W2, b2, out):
             load_h1(g, False)
         for x in range(NT):
             load_adj(x)
-            if x == 3:
+            if x == 4:
                 load_w2(4, 4)
 
         def warm_up():
@@ -304,7 +304,7 @@ def tile_gcnlayer_pa_kernel(tc, h1, adj, W2, b2, out):
         blocks = [(nh, g, q) for nh in range(2) for g in range(NG) for q in range(4)]
         sums_after = {}
         for x in range(NT):
-            sums_after.setdefault(max(-1, (30 + 17 * x) // 10), []).append(x)
+            sums_after.setdefault(max(-1, (40 + 17 * x) // 10), []).append(x)
 
         def sums(b):
             for x in sums_after.get(b, []):
@@ -393,7 +393,7 @@ def tile_gcnlayer_pa_kernel(tc, h1, adj, W2, b2, out):
                 if x >= early:
                     flip_adj(x, 0)
                 flip_adj(x, 1)
-            parts = [(0, 512), (512, 1024)] if x < NT else [(0, 512), (512, 768), (768, 1024)]
+            parts = [(0, 512), (512, 1024)] if x < NT else [(0, 512), (512, 768), (768, 896), (896, 1024)]
             for lo, hi in parts:
                 propagate(x - 1, lo, hi, range(2 if x - 1 < pre else 0, NG))
             if x < NT:

from contextlib import ExitStack

import concourse.mybir as mybir
from concourse.masks import make_identity

F32 = mybir.dt.float32
BF16 = mybir.dt.bfloat16
U32 = mybir.dt.uint32
U8 = mybir.dt.uint8
FP8X4 = mybir.dt.float8_e4m3fn_x4
ACT = mybir.ActivationFunctionType
ALU = mybir.AluOpType

P = 128
N_NODES = 2048
HID = 512
OUT_F = 1024
NT = N_NODES // P
NG = NT // 4
FOLD_W = 128
N_FOLD = 10
FOLDED = FOLD_W * N_FOLD

FLOPS = 2 * N_NODES * HID * OUT_F + 2 * N_NODES * N_NODES * OUT_F


def tile_gcnlayer_pa_kernel(tc, h1, adj, W2, b2, out):
    nc = tc.nc
    with ExitStack() as ctx:
        keep = ctx.enter_context(tc.tile_pool(name="keep", bufs=1))
        wide = ctx.enter_context(tc.tile_pool(name="wide", bufs=3))
        grp = ctx.enter_context(tc.tile_pool(name="grp", bufs=4))
        spool = ctx.enter_context(tc.tile_pool(name="spool", bufs=5))
        cpool = ctx.enter_context(tc.tile_pool(name="cpool", bufs=4))
        opool = ctx.enter_context(tc.tile_pool(name="opool", bufs=3))
        ps_t = ctx.enter_context(tc.psum_pool(name="ps_t", bufs=4))
        ps_a = ctx.enter_context(tc.psum_pool(name="ps_a", bufs=4))
        ctx.enter_context(tc.manual_schedule())

        warm = keep.tile([P, 1], F32)
        warm2 = keep.tile([P, 1], F32)
        ident = keep.tile([P, P], F32)
        ident_b = keep.tile([P, P], BF16)
        w2n = keep.tile([P, (OUT_F // P) * HID], BF16)
        h1n = keep.tile([P, NT * HID], BF16)
        bias = keep.tile([P, OUT_F], F32)
        b_row = keep.tile([P, OUT_F], BF16)
        ones_w = keep.tile([P, 512], BF16)
        adj_sb = keep.tile([P, NT, N_NODES], BF16)
        w2c = keep.tile([P, OUT_F], U32, align_bytes=256)
        w2s = keep.tile([P, OUT_F], U8, align_bytes=256)
        h1c = keep.tile([P, N_NODES], U32, align_bytes=256)
        h1s = keep.tile([P, N_NODES], U8, align_bytes=256)
        hc = keep.tile([P, NG * OUT_F], U32, align_bytes=256)
        hs = keep.tile([P, NG * OUT_F], U8, align_bytes=256)
        deg_p = keep.tile([P, NT], F32)
        deg_s = keep.tile([P, NT], F32)
        r = keep.tile([P, NT], F32)
        r_row = keep.tile([P, N_NODES], F32)
        junk = keep.tile([P, N_NODES - FOLDED], BF16)
        junk2 = keep.tile([P, FOLD_W], BF16)
        adj_i = keep.tile([P, NT, P], F32)
        live = {}

        nc.vector.memset(ones_w[:], 1.0)
        nc.vector.memset(b_row[:], 0.0)
        nc.vector.memset(warm[:], 1.0)
        nc.scalar.activation(out=warm2[:], in_=warm[:], func=ACT.Abs_reciprocal_sqrt)
        make_identity(nc, ident[:])
        make_identity(nc, ident_b[:])

        def load_h1(g, halves):
            dst = h1n[:, 4 * g * HID : 4 * (g + 1) * HID].rearrange("p (u e k) -> p u e k", u=2, e=2)
            src = h1[4 * g * P : 4 * (g + 1) * P, :].rearrange("(u p e) k -> p u e k", p=P, e=2)
            for us in [slice(0, 1), slice(1, 2)] if halves else [slice(0, 2)]:
                nc.sync.dma_start(out=dst[:, us], in_=src[:, us])

        def load_w2(first, count):
            nc.sync.dma_start(
                out=w2n[:, first * HID : (first + count) * HID].rearrange("p (c k) -> p c k", k=HID),
                in_=W2[first * P : (first + count) * P, :].rearrange("(c p) k -> p c k", p=P),
            )

        def load_adj(x):
            nc.sync.dma_start(out=adj_sb[:, x, :], in_=adj[x * P : (x + 1) * P, :])

        load_h1(0, True)
        nc.sync.dma_start(out=b_row[0:1, :], in_=b2.unsqueeze(0))
        load_w2(0, 1)
        load_w2(1, 1)
        load_w2(2, 2)
        for g in range(1, NG):
            load_h1(g, False)
        for x in range(NT):
            load_adj(x)
            if x == 4:
                load_w2(4, 4)

        def warm_up():
            pw = ps_a.tile([P, 512], F32, tag="acc", name="pw")
            for c in range(6):
                nc.tensor.matmul(out=pw[:], lhsT=ones_w[:, 0:P], rhs=ones_w[:], start=True, stop=True)

        def spread_bias(nh, on_vector):
            pb = ps_a.tile([P, 512], F32, tag="acc", name="pb")
            cols = slice(512 * nh, 512 * (nh + 1))
            nc.tensor.matmul(out=pb[:], lhsT=ones_w[:, 0:P], rhs=b_row[:, cols], start=True, stop=True)
            if on_vector:
                nc.vector.tensor_copy(out=bias[:, cols], in_=pb[:])
            else:
                nc.scalar.copy(out=bias[:, cols], in_=pb[:])

        def flip_rows(src_words, first_tile, count, dst_words, on_vector):
            tp = ps_t.tile([P, 2 * count, P], F32, tag="tp", name="tp")
            for c in range(count):
                for u in range(2):
                    col = (first_tile + c) * (HID // 2) + u * P
                    nc.tensor.transpose(tp[:, 2 * c + u, :], src_words[:, col : col + P], ident[:])
            dst = dst_words.rearrange("p (c n u) -> p c n u", c=count, u=2)
            src = tp[:].rearrange("p (c u) n -> p c n u", c=count)
            if on_vector:
                nc.vector.tensor_copy(out=dst, in_=src)
            else:
                nc.scalar.copy(out=dst, in_=src)

        def flip_w2(first, count):
            w2g_room = wide.tile([P, 2 * 512], BF16, tag="w2g", name="w2g", align_bytes=64)
            w2g = w2g_room[:, 0 : 512 * count]
            live["w2g", first] = w2g
            flip_rows(w2n[:].bitcast(F32), first, count, w2g.bitcast(F32), False)

        def quant_w2(first, count):
            cols = slice(P * first, P * (first + count))
            nc.vector.quantize_mx(out=w2c[:, cols].bitcast(FP8X4), scales=w2s[:, cols], in_=live["w2g", first])

        def flip_h1(g, share):
            h1g = grp.tile([P, 4 * 512], BF16, tag="grp", name="h1g", align_bytes=64)
            live["h1g", g] = h1g
            for b in range(2):
                flip_rows(
                    h1n[:].bitcast(F32), 4 * g + 2 * b, 2, h1g[:].bitcast(F32)[:, 512 * b : 512 * (b + 1)], share and b == 1
                )

        def quant_h1(g):
            nc.vector.quantize_mx(
                out=h1c[:, 512 * g : 512 * (g + 1)].bitcast(FP8X4),
                scales=h1s[:, 512 * g : 512 * (g + 1)],
                in_=live["h1g", g][:],
            )

        def project(b):
            nh, g, q = blocks[b]
            nb = 4 * nh + q
            acc = ps_a.tile([P, 4, P], F32, tag="acc", name="acc1")
            live["prj", b] = acc
            for t in range(4):
                x = 4 * g + t
                nc.tensor.matmul_mx(
                    out=acc[:, t, :],
                    lhsT=h1c[:, x * P : (x + 1) * P].bitcast(FP8X4),
                    lhsT_scale=h1s[:, x * P : (x + 1) * P],
                    rhs=w2c[:, nb * P : (nb + 1) * P].bitcast(FP8X4),
                    rhs_scale=w2s[:, nb * P : (nb + 1) * P],
                    start=True,
                    stop=True,
                )

        def add_bias(b):
            nh, g, q = blocks[b]
            nb = 4 * nh + q
            if q == 0:
                live["hg", nh, g] = wide.tile([P, 4 * 512], BF16, tag="wide", name="hg", align_bytes=64)
            nc.vector.tensor_tensor(
                out=live["hg", nh, g][:, 512 * q : 512 * (q + 1)].rearrange("p (n t) -> p n t", t=4),
                in0=live["prj", b][:].rearrange("p t n -> p n t"),
                in1=bias[:, nb * P : (nb + 1) * P].unsqueeze(2).to_broadcast([P, P, 4]),
                op=ALU.add,
            )

        def quant_h(nh, g):
            col = OUT_F * g + 512 * nh
            nc.vector.quantize_mx(
                out=hc[:, col : col + 512].bitcast(FP8X4),
                scales=hs[:, col : col + 512],
                in_=live["hg", nh, g][:],
            )

        def inverse_root(x):
            nc.scalar.activation(
                out=r[:, x : x + 1],
                in_=deg_p[:, x : x + 1],
                func=ACT.Abs_reciprocal_sqrt,
                bias=deg_s[:, x : x + 1],
            )

        def row_sums(x):
            fold = ps_t.tile([P, FOLD_W], F32, tag="tp", name="fold")
            for c in range(N_FOLD):
                nc.tensor.matmul(
                    out=fold[:],
                    lhsT=ident_b[:],
                    rhs=adj_sb[:, x, c * FOLD_W : (c + 1) * FOLD_W],
                    start=(c == 0),
                    stop=(c == N_FOLD - 1),
                )
            nc.scalar.activation(
                out=junk[:],
                in_=adj_sb[:, x, FOLDED:N_NODES],
                func=ACT.Copy,
                bias=1.0 / (N_NODES - FOLDED),
                accum_out=deg_s[:, x : x + 1],
            )
            if x > 0:
                inverse_root(x - 1)
            nc.scalar.activation(
                out=junk2[:], in_=fold[:], func=ACT.Copy, accum_out=deg_p[:, x : x + 1]
            )

        def add_loops(x):
            nc.gpsimd.tensor_tensor(
                out=adj_i[:, x, :], in0=adj_sb[:, x, x * P : (x + 1) * P], in1=ident[:], op=ALU.add
            )

        def spread(g):
            sp = ps_t.tile([P, 4, P], F32, tag="tp", name="sp")
            for t in range(4):
                x = 4 * g + t
                nc.tensor.transpose(sp[:, t, :], r[:, x : x + 1].to_broadcast([P, P]), ident[:])
            nc.scalar.copy(
                out=r_row[:, 512 * g : 512 * (g + 1)].rearrange("p (t n) -> p t n", t=4), in_=sp[:]
            )

        def scale_piece(x, lo, hi, src):
            nc.vector.scalar_tensor_tensor(
                out=live["scaled", x][:, lo:hi],
                in0=src,
                scalar=r[:, x : x + 1],
                in1=r_row[:, lo:hi],
                op0=ALU.mult,
                op1=ALU.mult,
            )

        def scale(x, lo, hi):
            if lo == 0:
                live["scaled", x] = spool.tile([P, N_NODES], BF16, tag="scaled", name="scaled", align_bytes=64)
            d0 = max(lo, min(hi, x * P))
            d1 = max(lo, min(hi, (x + 1) * P))
            if d0 > lo:
                scale_piece(x, lo, d0, adj_sb[:, x, lo:d0])
            if d1 > d0:
                scale_piece(x, d0, d1, adj_i[:, x, :])
            if hi > d1:
                scale_piece(x, d1, hi, adj_sb[:, x, d1:hi])

        def flip_adj(x, b):
            words = live["scaled", x][:].bitcast(F32)
            tp = ps_t.tile([P, 4, P], F32, tag="tp", name="tpa")
            live["tp", x, b] = tp
            for c in range(4):
                col = (4 * b + c) * P
                nc.tensor.transpose(tp[:, c, :], words[:, col : col + P], ident[:])

        def regroup(x, b):
            if b == 0:
                live["ag", x] = grp.tile([P, 4 * 512], BF16, tag="grp", name="ag", align_bytes=64)
            nc.scalar.copy(
                out=live["ag", x][:].bitcast(F32)[:, 512 * b : 512 * (b + 1)].rearrange("p (g i u) -> p g i u", g=2, u=2),
                in_=live["tp", x, b][:].rearrange("p (g u) i -> p g i u", g=2),
            )

        def quant_adj(x, lo, hi):
            if lo == 0:
                live["ac", x] = cpool.tile([P, 512], U32, tag="ac", name="ac", align_bytes=256)
                live["asc", x] = cpool.tile([P, 512], U8, tag="asc", name="asc", align_bytes=256)
            nc.vector.quantize_mx(
                out=live["ac", x][:, lo // 4 : hi // 4].bitcast(FP8X4),
                scales=live["asc", x][:, lo // 4 : hi // 4],
                in_=live["ag", x][:, lo:hi],
            )

        def propagate(x, lo, hi, passes):
            if passes[0] == 0:
                live["acc", x, lo] = ps_a.tile([P, hi - lo], F32, tag="acc", name="acc2")
            for g in passes:
                cols = slice(OUT_F * g + lo, OUT_F * g + hi)
                nc.tensor.matmul_mx(
                    out=live["acc", x, lo][:],
                    lhsT=live["ac", x][:, g * P : (g + 1) * P].bitcast(FP8X4),
                    lhsT_scale=live["asc", x][:, g * P : (g + 1) * P],
                    rhs=hc[:, cols].bitcast(FP8X4),
                    rhs_scale=hs[:, cols],
                    start=(g == 0),
                    stop=(g == NG - 1),
                )

        def drain(x, lo, hi):
            if lo == 0:
                live["ot", x] = opool.tile([P, OUT_F], F32, tag="ot", name="ot")
            nc.scalar.copy(out=live["ot", x][:, lo:hi], in_=live["acc", x, lo][:])

        def store(x, lo, hi):
            nc.sync.dma_start(out=out[x * P : (x + 1) * P, lo:hi], in_=live["ot", x][:, lo:hi])

        blocks = [(nh, g, q) for nh in range(2) for g in range(NG) for q in range(4)]
        sums_after = {}
        for x in range(NT):
            sums_after.setdefault(max(-1, (40 + 17 * x) // 10), []).append(x)

        def sums(b):
            for x in sums_after.get(b, []):
                row_sums(x)
                add_loops(x)
                if x == 4:
                    flip_w2(4, 2)
                    flip_w2(6, 2)
                    spread_bias(1, False)
                if x in {12: 0, 15: 1}:
                    flip_adj({12: 0, 15: 1}[x], 0)
                    regroup({12: 0, 15: 1}[x], 0)
                if x % 4 == 0 and x > 0:
                    spread(x // 4 - 1)

        done = {}

        def step(b):
            nh, g, q = blocks[b]
            for gf in {2: [2, 3]}.get(b, []):
                flip_h1(gf, False)
            if nh == 0 and q == 2 and g < NG - 1:
                quant_h1(g + 1)
            if b == 13:
                quant_w2(4, 2)
            if b == 15:
                quant_w2(6, 2)
            if b == 0:
                add_bias(0)
                quant_w2(1, 1)
                project(1)
                quant_w2(2, 2)
                project(2)
            else:
                if b + 2 < 32:
                    project(b + 2)
                add_bias(b)
            sums(b)
            if q == 1 and b > 1:
                quant_h(blocks[b - 2][0], blocks[b - 2][1])
            for x, lo, hi in {14:[(0,0,512)],16:[(1,0,512)],18:[(2,0,512)],20:[(3,0,512)],22:[(0,512,1024)],25:[(1,512,1024)]}.get(b, []):
                scale(x, lo, hi)
                done[x] = hi
            if b in {}:
                flip_adj({}[b], 0)
                regroup({}[b], 0)
            if b in {28: 0, 31: 1}:
                quant_adj({28: 0, 31: 1}[b], 0, 1024)

        warm_up()
        flip_h1(0, True)
        flip_w2(0, 1)
        quant_h1(0)
        quant_w2(0, 1)
        spread_bias(0, True)
        flip_w2(1, 1)
        flip_w2(2, 2)
        project(0)
        for g in [1]:
            flip_h1(g, False)
        sums(-1)
        for b in range(32):
            step(b)
        inverse_root(NT - 1)
        early = len([x for x in done if done[x] >= 1024])
        pre = len({28: 0, 31: 1})
        for x in range(pre, early):
            flip_adj(x, 0)
            regroup(x, 0)
        propagate(0, 0, 512, range(2))
        propagate(0, 512, 1024, range(2))
        spread(NG - 1)
        propagate(1, 0, 512, range(2))
        propagate(1, 512, 1024, range(2))
        if done[0] < 1536:
            scale(0, done[0], 1536)
        quant_h(1, NG - 1)
        scale(0, 1536, N_NODES)
        flip_adj(0, 1)
        regroup(0, 1)
        for x in range(1, NT + 1):
            if x < NT:
                scale(x, done.get(x, 0), N_NODES)
            quant_adj(x - 1, 1024 if x - 1 < pre else 0, N_NODES)
            if x < NT:
                if x >= early:
                    flip_adj(x, 0)
                flip_adj(x, 1)
            parts = [(0, 512), (512, 1024)] if x < NT else [(0, 512), (512, 768), (768, 896), (896, 1024)]
            for lo, hi in parts:
                propagate(x - 1, lo, hi, range(2 if x - 1 < pre else 0, NG))
            if x < NT:
                if x >= early:
                    regroup(x, 0)
                regroup(x, 1)
            for lo, hi in parts:
                drain(x - 1, lo, hi)
                if x == NT:
                    store(x - 1, lo, hi)
            if x < NT:
                store(x - 1, 0, OUT_F)
